import numpy as np
import ml_dtypes


def mxq(x, axis, fmt="e4m3"):
    dtype, down = {"e4m3": (ml_dtypes.float8_e4m3fn, 7), "e5m2": (ml_dtypes.float8_e5m2, 14)}[fmt]
    v = np.moveaxis(np.asarray(x, np.float32).astype(ml_dtypes.bfloat16).astype(np.float64), axis, -1)
    blocks = v.reshape(v.shape[:-1] + (-1, 32))
    amax = np.abs(blocks).max(-1, keepdims=True)
    byte = np.maximum(np.where(amax > 0, np.frexp(amax)[1] - 1 + 127, 0) - down, 1)
    scale = np.exp2(byte - 127.0)
    codes = (blocks / scale).astype(np.float32).astype(dtype).astype(np.float64)
    return np.moveaxis((codes * scale).reshape(v.shape), -1, axis)


WIDE = False


def mx_kscale(k):
    if not WIDE:
        return np.ones(k)
    levels = np.array([10, -10, 5, -5, 0])
    a = np.random.permutation(np.resize(levels, k // 512 * 4)).reshape(k // 512, 4)
    idx = np.arange(k)
    return np.exp2(a[idx // 512, idx % 128 // 32])


BF16 = ml_dtypes.bfloat16


def bf(x):
    return np.asarray(x, np.float32).astype(BF16)


def f64(x):
    return np.asarray(x).astype(np.float64)


C, I, T, R, D = 8, 8, 128, 512, 256


def sigmoid(v):
    return 1.0 / (1.0 + np.exp(-v))


def setup_inputs():
    s = mx_kscale(D + D)[D:]
    u = np.concatenate([np.ones(D), s])[:, None]
    return {"query": bf(np.random.standard_normal((C, I, T, D)) * 0.5),
            "wc": bf(np.random.standard_normal((C, I, T, D)) * 6.0 / np.sqrt(R) * s),
            "w_lin": bf(np.random.standard_normal((D + D, D)) * 1.5 / np.sqrt(D) / u),
            "b_lin": bf(np.random.standard_normal(D) * 0.2),
            "w_gate": bf(np.random.standard_normal((D + D, D)) * 1.5 / np.sqrt(D) / u),
            "b_gate": bf(np.random.standard_normal(D) * 0.2)}


def reference(query, wc, w_lin, b_lin, w_gate, b_gate):
    q = f64(query)
    cat = mxq(np.concatenate([q, f64(wc)], axis=-1), 3, "e4m3")
    upd = np.tanh((cat @ mxq(f64(w_lin), 0, "e4m3")) + f64(b_lin))
    gate = sigmoid((cat @ mxq(f64(w_gate), 0, "e4m3")) + f64(b_gate))
    return q * gate + upd * (1.0 - gate)

@@ -1,0 +1,185 @@
+from contextlib import ExitStack
+
+import concourse.bass as bass
+import concourse.mybir as mybir
+import concourse.tile as tile
+from concourse.masks import make_identity
+
+F32 = mybir.dt.float32
+BF16 = mybir.dt.bfloat16
+U32 = mybir.dt.uint32
+U8 = mybir.dt.uint8
+FP8X4 = mybir.dt.float8_e4m3fn_x4
+ACT = mybir.ActivationFunctionType
+ALU = mybir.AluOpType
+
+P = 128
+D = 256
+TOK = 8192
+JP = TOK // P
+TPG = 4
+NG = JP // TPG
+FLOPS = 2 * TOK * 512 * 512
+
+
+def tile_scan_pb_t_kernel(tc, query, wc, w_lin, b_lin, w_gate, b_gate, out):
+    nc = tc.nc
+    q_v = query.flatten_outer_dims().rearrange("(p j) d -> p j d", j=JP)
+    c_v = wc.flatten_outer_dims().rearrange("(p j) d -> p j d", j=JP)
+    o_v = out.flatten_outer_dims().rearrange("(p j) d -> p j d", j=JP)
+
+    with ExitStack() as ctx:
+        ctx.enter_context(tc.manual_schedule())
+        const = ctx.enter_context(tc.tile_pool(name="const", bufs=1))
+        xpool = ctx.enter_context(tc.tile_pool(name="xpool", bufs=NG))
+        opool = ctx.enter_context(tc.tile_pool(name="opool", bufs=NG))
+        gpool = ctx.enter_context(tc.tile_pool(name="gpool", bufs=2))
+        kpool = ctx.enter_context(tc.tile_pool(name="kpool", bufs=3))
+        apool = ctx.enter_context(tc.tile_pool(name="apool", bufs=3))
+        npool = ctx.enter_context(tc.tile_pool(name="npool", bufs=2))
+        ps_ct = ctx.enter_context(tc.psum_pool(name="ps_ct", bufs=2))
+        ps_z = ctx.enter_context(tc.psum_pool(name="ps_z", bufs=4))
+        ps_b = ctx.enter_context(tc.psum_pool(name="ps_b", bufs=1))
+
+        ident = const.tile([P, P], F32)
+        make_identity(nc, ident[:])
+        bz = const.tile([P, P], BF16)
+        nc.vector.memset(bz[:], 0.0)
+
+        xs = []
+        for g in range(NG):
+            x_t = xpool.tile([P, TPG, 2 * D], BF16, tag="x")
+            xs.append(x_t)
+
+        def load_x(g):
+            js = slice(g * TPG, (g + 1) * TPG)
+            nc.sync.dma_start(out=xs[g][:, :, 0:D], in_=q_v[:, js, :])
+            nc.sync.dma_start(out=xs[g][:, :, D : 2 * D], in_=c_v[:, js, :])
+
+        load_x(0)
+        w_raw = const.tile([P, 2, 4, D], BF16)
+        nc.scalar.dma_start(out=w_raw[:, 0], in_=w_lin.rearrange("(p t) c -> p t c", t=4))
+        nc.scalar.dma_start(out=w_raw[:, 1], in_=w_gate.rearrange("(p t) c -> p t c", t=4))
+        nc.scalar.dma_start(out=bz[0:2, :], in_=b_lin.rearrange("(r c) -> r c", r=2))
+        nc.scalar.dma_start(out=bz[2:4, :], in_=b_gate.rearrange("(r c) -> r c", r=2))
+        for g in range(1, NG):
+            load_x(g)
+
+        st = {}
+
+        def stage_a(g):
+            x32 = xs[g][:].bitcast(F32).rearrange("p j (m e) -> p j e m", e=2)
+            cts = []
+            for s in range(2):
+                ct = ps_ct.tile([P, 2, 2, P], F32, tag="ct")
+                for a in range(2):
+                    for e in range(2):
+                        nc.tensor.transpose(ct[:, a, e, :], x32[:, 2 * s + a, e, :], ident[:])
+                cts.append(ct)
+            st[("ct", g)] = cts
+
+        def stage_b(g):
+            gr = gpool.tile([P, TPG * P * 4], BF16, tag="gr", align_bytes=64)
+            g32 = gr[:].bitcast(F32)
+            for s in range(2):
+                dst = g32[:, s * 512 : (s + 1) * 512].rearrange("p (a n e) -> p a n e", a=2, e=2)
+                src = st[("ct", g)][s][:].rearrange("p a e n -> p a n e")
+                nc.scalar.copy(out=dst, in_=src)
+            st[("gr", g)] = gr
+
+        def stage_c(g):
+            codes = kpool.tile([P, TPG * P], U32, tag="codes", align_bytes=64)
+            sc = kpool.tile([P, TPG * P], U8, tag="sc", align_bytes=64)
+            nc.vector.quantize_mx(out=codes[:].bitcast(FP8X4), scales=sc[:], in_=st[("gr", g)][:])
+            st[("k", g)] = (codes, sc)
+
+        w_grp = const.tile([P, 2, D, 4], BF16, align_bytes=64)
+        w_codes = const.tile([P, 2 * D], U32, align_bytes=64)
+        w_sc = const.tile([P, 2 * D], U8, align_bytes=64)
+        bz32 = const.tile([P, P], F32)
+        bias4 = const.tile([P, 4], F32)
+
+        stage_a(0)
+        stage_b(0)
+        nc.vector.tensor_copy(out=bz32[:], in_=bz[:])
+        b_ps = ps_b.tile([P, P], F32, tag="hb")
+        nc.tensor.transpose(b_ps[:], bz32[:], ident[:])
+        nc.vector.tensor_copy(out=w_grp[:], in_=w_raw[:].rearrange("p w t c -> p w c t"))
+        nc.vector.tensor_copy(out=bias4[:, 0:2], in_=b_ps[:, 0:2])
+        nc.vector.tensor_scalar_mul(out=bias4[:, 2:4], in0=b_ps[:, 2:4], scalar1=-1.0)
+        nc.vector.quantize_mx(
+            out=w_codes[:].bitcast(FP8X4), scales=w_sc[:], in_=w_grp[:].rearrange("p w c t -> p (w c t)")
+        )
+        stage_c(0)
+        stage_a(1)
+        stage_b(1)
+        stage_c(1)
+
+        order = [(2, True, 0), (0, False, 0), (3, True, 1), (1, False, 1)]
+
+        def stage_de(g):
+            codes, sc = st[("k", g)]
+            h_t = apool.tile([P, 2, 512], F32, tag="hT")
+            u_t = apool.tile([P, 2, 512], F32, tag="uT")
+            zs = []
+            for (c, gate, hf) in order:
+                z = ps_z.tile([P, 512], F32, tag="z")
+                cs = slice(c * P, (c + 1) * P)
+                nc.tensor.matmul_mx(
+                    out=z[:],
+                    lhsT=w_codes[:, cs].bitcast(FP8X4),
+                    lhsT_scale=w_sc[:, cs],
+                    rhs=codes[:].bitcast(FP8X4),
+                    rhs_scale=sc[:],
+                    start=True,
+                    stop=True,
+                )
+                zs.append(z)
+            for i, (c, gate, hf) in enumerate(order):
+                if gate:
+                    nc.scalar.activation(
+                        out=h_t[:, hf, :], in_=zs[i][:], func=ACT.Sigmoid, bias=bias4[:, c : c + 1], scale=-1.0
+                    )
+                else:
+                    nc.scalar.activation(
+                        out=u_t[:, hf, :], in_=zs[i][:], func=ACT.Tanh, bias=bias4[:, c : c + 1], scale=1.0
+                    )
+            w_t = apool.tile([P, 2, 512], F32, tag="wT")
+            for hf in range(2):
+                nc.gpsimd.tensor_tensor(out=w_t[:, hf, :], in0=h_t[:, hf, :], in1=u_t[:, hf, :], op=ALU.mult)
+            st[("hw", g)] = (h_t, w_t)
+            o_t = opool.tile([P, TPG, D], F32, tag="o")
+            st[("o", g)] = o_t
+
+        def stage_hi(g, s):
+            h_t, w_t = st[("hw", g)]
+            o_t = st[("o", g)]
+            hb = ps_b.tile([P, 2, D], F32, tag="hb")
+            wb = ps_b.tile([P, 2, D], F32, tag="wb")
+            for (dst, src) in ((hb, h_t), (wb, w_t)):
+                for a in range(2):
+                    for hf in range(2):
+                        t0 = (2 * s + a) * P
+                        nc.tensor.transpose(dst[:, a, hf * P : (hf + 1) * P], src[:, hf, t0 : t0 + P], ident[:])
+            na = npool.tile([P, 2, D], F32, tag="na")
+            nc.vector.scalar_tensor_tensor(
+                out=na[:], in0=hb[:], scalar=-1.0, in1=xs[g][:, 2 * s : 2 * s + 2, 0:D], op0=ALU.add, op1=ALU.mult
+            )
+            nc.vector.tensor_tensor(out=o_t[:, 2 * s : 2 * s + 2, :], in0=wb[:], in1=na[:], op=ALU.subtract)
+
+        def stage_j(g):
+            nc.sync.dma_start(out=o_v[:, g * TPG : (g + 1) * TPG, :], in_=st[("o", g)][:])
+
+        for p in range(NG + 1):
+            if p < NG:
+                stage_de(p)
+            if p >= 1:
+                stage_hi(p - 1, 0)
+            if p + 2 < NG:
+                stage_a(p + 2)
+                stage_b(p + 2)
+            if p >= 1:
+                stage_hi(p - 1, 1)
+                stage_j(p - 1)
+            if p + 2 < NG:
+                stage_c(p + 2)

@@ -1,8 +1,6 @@
 from contextlib import ExitStack
 
-import concourse.bass as bass
 import concourse.mybir as mybir
-import concourse.tile as tile
 from concourse.masks import make_identity
 
 F32 = mybir.dt.float32
@@ -19,20 +17,21 @@ TOK = 8192
 JP = TOK // P
 TPG = 4
 NG = JP // TPG
+NH = 2 * NG
 FLOPS = 2 * TOK * 512 * 512
 
 
 def tile_scan_pb_t_kernel(tc, query, wc, w_lin, b_lin, w_gate, b_gate, out):
     nc = tc.nc
-    q_v = query.flatten_outer_dims().rearrange("(p j) d -> p j d", j=JP)
-    c_v = wc.flatten_outer_dims().rearrange("(p j) d -> p j d", j=JP)
+    q_v = query.flatten_outer_dims().rearrange("(p j) (u c) -> p j u c", j=JP, u=2)
+    c_v = wc.flatten_outer_dims().rearrange("(p j) (u c) -> p j u c", j=JP, u=2)
     o_v = out.flatten_outer_dims().rearrange("(p j) d -> p j d", j=JP)
 
     with ExitStack() as ctx:
         ctx.enter_context(tc.manual_schedule())
         const = ctx.enter_context(tc.tile_pool(name="const", bufs=1))
         xpool = ctx.enter_context(tc.tile_pool(name="xpool", bufs=NG))
-        opool = ctx.enter_context(tc.tile_pool(name="opool", bufs=NG))
+        opool = ctx.enter_context(tc.tile_pool(name="opool", bufs=NH))
         gpool = ctx.enter_context(tc.tile_pool(name="gpool", bufs=2))
         kpool = ctx.enter_context(tc.tile_pool(name="kpool", bufs=3))
         apool = ctx.enter_context(tc.tile_pool(name="apool", bufs=3))
@@ -48,18 +47,22 @@ def tile_scan_pb_t_kernel(tc, query, wc, w_lin, b_lin, w_gate, b_gate, out):
 
         xs = []
         for g in range(NG):
-            x_t = xpool.tile([P, TPG, 2 * D], BF16, tag="x")
+            x_t = xpool.tile([P, TPG, 2, 2, P], BF16, tag="x")
             xs.append(x_t)
 
         def load_x(g):
             js = slice(g * TPG, (g + 1) * TPG)
-            nc.sync.dma_start(out=xs[g][:, :, 0:D], in_=q_v[:, js, :])
-            nc.sync.dma_start(out=xs[g][:, :, D : 2 * D], in_=c_v[:, js, :])
+            nc.sync.dma_start(out=xs[g][:, :, :, 0, :], in_=q_v[:, js, :, :])
+            nc.sync.dma_start(out=xs[g][:, :, :, 1, :], in_=c_v[:, js, :, :])
 
         load_x(0)
         w_raw = const.tile([P, 2, 4, D], BF16)
-        nc.scalar.dma_start(out=w_raw[:, 0], in_=w_lin.rearrange("(p t) c -> p t c", t=4))
-        nc.scalar.dma_start(out=w_raw[:, 1], in_=w_gate.rearrange("(p t) c -> p t c", t=4))
+        for i, w in enumerate((w_lin, w_gate)):
+            w_v = w.rearrange("(s u m e) c -> s m u (e c)", s=2, u=2, e=2)
+            for s in range(2):
+                nc.scalar.dma_start(
+                    out=w_raw[64 * s : 64 * s + 64, i].rearrange("m (u e) c -> m u (e c)", u=2), in_=w_v[s]
+                )
         nc.scalar.dma_start(out=bz[0:2, :], in_=b_lin.rearrange("(r c) -> r c", r=2))
         nc.scalar.dma_start(out=bz[2:4, :], in_=b_gate.rearrange("(r c) -> r c", r=2))
         for g in range(1, NG):
@@ -67,27 +70,25 @@ def tile_scan_pb_t_kernel(tc, query, wc, w_lin, b_lin, w_gate, b_gate, out):
 
         st = {}
 
-        def stage_a(g):
-            x32 = xs[g][:].bitcast(F32).rearrange("p j (m e) -> p j e m", e=2)
-            cts = []
-            for s in range(2):
-                ct = ps_ct.tile([P, 2, 2, P], F32, tag="ct")
-                for a in range(2):
-                    for e in range(2):
-                        nc.tensor.transpose(ct[:, a, e, :], x32[:, 2 * s + a, e, :], ident[:])
-                cts.append(ct)
-            st[("ct", g)] = cts
+        def transpose_in(a):
+            g, s = divmod(a, 2)
+            x32 = xs[g][:].bitcast(F32).rearrange("p j u s w -> p j u (s w)")
+            ct = ps_ct.tile([P, 2, 2, P], F32, tag="ct")
+            for t in range(2):
+                for u in range(2):
+                    nc.tensor.transpose(ct[:, t, u, :], x32[:, 2 * s + t, u, :], ident[:])
+            st[("ct", a)] = ct
 
-        def stage_b(g):
-            gr = gpool.tile([P, TPG * P * 4], BF16, tag="gr", align_bytes=64)
-            g32 = gr[:].bitcast(F32)
-            for s in range(2):
-                dst = g32[:, s * 512 : (s + 1) * 512].rearrange("p (a n e) -> p a n e", a=2, e=2)
-                src = st[("ct", g)][s][:].rearrange("p a e n -> p a n e")
-                nc.scalar.copy(out=dst, in_=src)
-            st[("gr", g)] = gr
+        def copy_in(a):
+            g, s = divmod(a, 2)
+            if s == 0:
+                gr = gpool.tile([P, TPG * P * 4], BF16, tag="gr", align_bytes=64)
+                st[("gr", g)] = gr
+            g32 = st[("gr", g)][:].bitcast(F32)
+            dst = g32[:, s * 512 : (s + 1) * 512].rearrange("p (t n u) -> p t n u", t=2, u=2)
+            nc.scalar.copy(out=dst, in_=st[("ct", a)][:].rearrange("p t u n -> p t n u"))
 
-        def stage_c(g):
+        def quantise(g):
             codes = kpool.tile([P, TPG * P], U32, tag="codes", align_bytes=64)
             sc = kpool.tile([P, TPG * P], U8, tag="sc", align_bytes=64)
             nc.vector.quantize_mx(out=codes[:].bitcast(FP8X4), scales=sc[:], in_=st[("gr", g)][:])
@@ -99,8 +100,10 @@ def tile_scan_pb_t_kernel(tc, query, wc, w_lin, b_lin, w_gate, b_gate, out):
         bz32 = const.tile([P, P], F32)
         bias4 = const.tile([P, 4], F32)
 
-        stage_a(0)
-        stage_b(0)
+        transpose_in(0)
+        transpose_in(1)
+        copy_in(0)
+        copy_in(1)
         nc.vector.tensor_copy(out=bz32[:], in_=bz[:])
         b_ps = ps_b.tile([P, P], F32, tag="hb")
         nc.tensor.transpose(b_ps[:], bz32[:], ident[:])
@@ -110,19 +113,22 @@ def tile_scan_pb_t_kernel(tc, query, wc, w_lin, b_lin, w_gate, b_gate, out):
         nc.vector.quantize_mx(
             out=w_codes[:].bitcast(FP8X4), scales=w_sc[:], in_=w_grp[:].rearrange("p w c t -> p (w c t)")
         )
-        stage_c(0)
-        stage_a(1)
-        stage_b(1)
-        stage_c(1)
+        quantise(0)
+        transpose_in(2)
+        copy_in(2)
+        transpose_in(3)
 
-        order = [(2, True, 0), (0, False, 0), (3, True, 1), (1, False, 1)]
-
-        def stage_de(g):
+        def product(k):
+            g, hf = divmod(k, 2)
             codes, sc = st[("k", g)]
-            h_t = apool.tile([P, 2, 512], F32, tag="hT")
-            u_t = apool.tile([P, 2, 512], F32, tag="uT")
+            if hf == 0:
+                h_t = apool.tile([P, 2, 512], F32, tag="hT")
+                u_t = apool.tile([P, 2, 512], F32, tag="uT")
+                w_t = apool.tile([P, 2, 512], F32, tag="wT")
+                st[("huw", g)] = (h_t, u_t, w_t)
+            h_t, u_t, w_t = st[("huw", g)]
             zs = []
-            for (c, gate, hf) in order:
+            for c in (2 + hf, hf):
                 z = ps_z.tile([P, 512], F32, tag="z")
                 cs = slice(c * P, (c + 1) * P)
                 nc.tensor.matmul_mx(
@@ -135,51 +141,38 @@ def tile_scan_pb_t_kernel(tc, query, wc, w_lin, b_lin, w_gate, b_gate, out):
                     stop=True,
                 )
                 zs.append(z)
-            for i, (c, gate, hf) in enumerate(order):
-                if gate:
-                    nc.scalar.activation(
-                        out=h_t[:, hf, :], in_=zs[i][:], func=ACT.Sigmoid, bias=bias4[:, c : c + 1], scale=-1.0
-                    )
-                else:
-                    nc.scalar.activation(
-                        out=u_t[:, hf, :], in_=zs[i][:], func=ACT.Tanh, bias=bias4[:, c : c + 1], scale=1.0
-                    )
-            w_t = apool.tile([P, 2, 512], F32, tag="wT")
-            for hf in range(2):
-                nc.gpsimd.tensor_tensor(out=w_t[:, hf, :], in0=h_t[:, hf, :], in1=u_t[:, hf, :], op=ALU.mult)
-            st[("hw", g)] = (h_t, w_t)
-            o_t = opool.tile([P, TPG, D], F32, tag="o")
-            st[("o", g)] = o_t
-
-        def stage_hi(g, s):
-            h_t, w_t = st[("hw", g)]
-            o_t = st[("o", g)]
-            hb = ps_b.tile([P, 2, D], F32, tag="hb")
-            wb = ps_b.tile([P, 2, D], F32, tag="wb")
-            for (dst, src) in ((hb, h_t), (wb, w_t)):
-                for a in range(2):
-                    for hf in range(2):
-                        t0 = (2 * s + a) * P
-                        nc.tensor.transpose(dst[:, a, hf * P : (hf + 1) * P], src[:, hf, t0 : t0 + P], ident[:])
-            na = npool.tile([P, 2, D], F32, tag="na")
-            nc.vector.scalar_tensor_tensor(
-                out=na[:], in0=hb[:], scalar=-1.0, in1=xs[g][:, 2 * s : 2 * s + 2, 0:D], op0=ALU.add, op1=ALU.mult
+            nc.scalar.activation(
+                out=h_t[:, hf, :], in_=zs[0][:], func=ACT.Sigmoid, bias=bias4[:, 2 + hf : 3 + hf], scale=-1.0
             )
-            nc.vector.tensor_tensor(out=o_t[:, 2 * s : 2 * s + 2, :], in0=wb[:], in1=na[:], op=ALU.subtract)
+            nc.scalar.activation(out=u_t[:, hf, :], in_=zs[1][:], func=ACT.Tanh, bias=bias4[:, hf : hf + 1], scale=1.0)
+            nc.gpsimd.tensor_tensor(out=w_t[:, hf, :], in0=h_t[:, hf, :], in1=u_t[:, hf, :], op=ALU.mult)
 
-        def stage_j(g):
-            nc.sync.dma_start(out=o_v[:, g * TPG : (g + 1) * TPG, :], in_=st[("o", g)][:])
+        def blend(m):
+            g, s = divmod(m, 2)
+            h_t, u_t, w_t = st[("huw", g)]
+            hb = ps_b.tile([P, 4, P], F32, tag="hb")
+            wb = ps_b.tile([P, 4, P], F32, tag="wb")
+            for (dst, src) in ((hb, h_t), (wb, w_t)):
+                for t in range(2):
+                    for hf in range(2):
+                        t0 = (2 * s + t) * P
+                        nc.tensor.transpose(dst[:, 2 * t + hf, :], src[:, hf, t0 : t0 + P], ident[:])
+            q_nat = xs[g][:].rearrange("p j u s c -> p (j u) s c")[:, 4 * s : 4 * s + 4, 0, :]
+            na = npool.tile([P, 4, P], F32, tag="na")
+            nc.vector.scalar_tensor_tensor(out=na[:], in0=hb[:], scalar=-1.0, in1=q_nat, op0=ALU.add, op1=ALU.mult)
+            o_t = opool.tile([P, 4, P], F32, tag="o")
+            nc.vector.tensor_tensor(out=o_t[:], in0=wb[:], in1=na[:], op=ALU.subtract)
+            j0 = g * TPG + 2 * s
+            nc.sync.dma_start(out=o_v[:, j0 : j0 + 2, :], in_=o_t[:].rearrange("p (t hf) c -> p t (hf c)", t=2))
 
-        for p in range(NG + 1):
-            if p < NG:
-                stage_de(p)
-            if p >= 1:
-                stage_hi(p - 1, 0)
-            if p + 2 < NG:
-                stage_a(p + 2)
-                stage_b(p + 2)
-            if p >= 1:
-                stage_hi(p - 1, 1)
-                stage_j(p - 1)
-            if p + 2 < NG:
-                stage_c(p + 2)
+        for k in range(NH + 3):
+            if k + 3 < NH:
+                copy_in(k + 3)
+            if k < NH:
+                product(k)
+            if k >= 3:
+                blend(k - 3)
+            if k + 4 < NH:
+                transpose_in(k + 4)
+            if k % 2 == 0 and (k + 2) // 2 < NG:
+                quantise((k + 2) // 2)

@@ -145,7 +145,11 @@ def tile_scan_pb_t_kernel(tc, query, wc, w_lin, b_lin, w_gate, b_gate, out):
                 out=h_t[:, hf, :], in_=zs[0][:], func=ACT.Sigmoid, bias=bias4[:, 2 + hf : 3 + hf], scale=-1.0
             )
             nc.scalar.activation(out=u_t[:, hf, :], in_=zs[1][:], func=ACT.Tanh, bias=bias4[:, hf : hf + 1], scale=1.0)
-            nc.gpsimd.tensor_tensor(out=w_t[:, hf, :], in0=h_t[:, hf, :], in1=u_t[:, hf, :], op=ALU.mult)
+
+        def gate_times_update(k):
+            g, hf = divmod(k, 2)
+            h_t, u_t, w_t = st[("huw", g)]
+            nc.vector.tensor_tensor(out=w_t[:, hf, :], in0=h_t[:, hf, :], in1=u_t[:, hf, :], op=ALU.mult)
 
         def blend(m):
             g, s = divmod(m, 2)
@@ -170,6 +174,8 @@ def tile_scan_pb_t_kernel(tc, query, wc, w_lin, b_lin, w_gate, b_gate, out):
                 copy_in(k + 3)
             if k < NH:
                 product(k)
+            if 1 <= k <= NH:
+                gate_times_update(k - 1)
             if k >= 3:
                 blend(k - 3)
             if k + 4 < NH:

@@ -36,9 +36,9 @@ def tile_scan_pb_t_kernel(tc, query, wc, w_lin, b_lin, w_gate, b_gate, out):
         kpool = ctx.enter_context(tc.tile_pool(name="kpool", bufs=3))
         apool = ctx.enter_context(tc.tile_pool(name="apool", bufs=3))
         npool = ctx.enter_context(tc.tile_pool(name="npool", bufs=2))
-        ps_ct = ctx.enter_context(tc.psum_pool(name="ps_ct", bufs=2))
-        ps_z = ctx.enter_context(tc.psum_pool(name="ps_z", bufs=4))
-        ps_b = ctx.enter_context(tc.psum_pool(name="ps_b", bufs=1))
+        ps_ct = ctx.enter_context(tc.psum_pool(name="ps_ct", bufs=1))
+        ps_z = ctx.enter_context(tc.psum_pool(name="ps_z", bufs=3))
+        ps_b = ctx.enter_context(tc.psum_pool(name="ps_b", bufs=2))
 
         ident = const.tile([P, P], F32)
         make_identity(nc, ident[:])
@@ -51,11 +51,14 @@ def tile_scan_pb_t_kernel(tc, query, wc, w_lin, b_lin, w_gate, b_gate, out):
             xs.append(x_t)
 
         def load_x(g):
-            js = slice(g * TPG, (g + 1) * TPG)
-            nc.sync.dma_start(out=xs[g][:, :, :, 0, :], in_=q_v[:, js, :, :])
-            nc.sync.dma_start(out=xs[g][:, :, :, 1, :], in_=c_v[:, js, :, :])
+            for s in range(2):
+                js = slice(g * TPG + 2 * s, g * TPG + 2 * s + 2)
+                nc.sync.dma_start(out=xs[g][:, 2 * s : 2 * s + 2, :, 0, :], in_=q_v[:, js, :, :])
+                nc.sync.dma_start(out=xs[g][:, 2 * s : 2 * s + 2, :, 1, :], in_=c_v[:, js, :, :])
 
         load_x(0)
+        nc.scalar.dma_start(out=bz[0:2, :], in_=b_lin.rearrange("(r c) -> r c", r=2))
+        nc.scalar.dma_start(out=bz[2:4, :], in_=b_gate.rearrange("(r c) -> r c", r=2))
         w_raw = const.tile([P, 2, 4, D], BF16)
         for i, w in enumerate((w_lin, w_gate)):
             w_v = w.rearrange("(s u m e) c -> s m u (e c)", s=2, u=2, e=2)
@@ -63,8 +66,6 @@ def tile_scan_pb_t_kernel(tc, query, wc, w_lin, b_lin, w_gate, b_gate, out):
                 nc.scalar.dma_start(
                     out=w_raw[64 * s : 64 * s + 64, i].rearrange("m (u e) c -> m u (e c)", u=2), in_=w_v[s]
                 )
-        nc.scalar.dma_start(out=bz[0:2, :], in_=b_lin.rearrange("(r c) -> r c", r=2))
-        nc.scalar.dma_start(out=bz[2:4, :], in_=b_gate.rearrange("(r c) -> r c", r=2))
         for g in range(1, NG):
             load_x(g)
 
@@ -79,14 +80,14 @@ def tile_scan_pb_t_kernel(tc, query, wc, w_lin, b_lin, w_gate, b_gate, out):
                     nc.tensor.transpose(ct[:, t, u, :], x32[:, 2 * s + t, u, :], ident[:])
             st[("ct", a)] = ct
 
-        def copy_in(a):
+        def copy_in(a, eng_copy):
             g, s = divmod(a, 2)
             if s == 0:
                 gr = gpool.tile([P, TPG * P * 4], BF16, tag="gr", align_bytes=64)
                 st[("gr", g)] = gr
             g32 = st[("gr", g)][:].bitcast(F32)
             dst = g32[:, s * 512 : (s + 1) * 512].rearrange("p (t n u) -> p t n u", t=2, u=2)
-            nc.scalar.copy(out=dst, in_=st[("ct", a)][:].rearrange("p t u n -> p t n u"))
+            eng_copy(out=dst, in_=st[("ct", a)][:].rearrange("p t u n -> p t n u"))
 
         def quantise(g):
             codes = kpool.tile([P, TPG * P], U32, tag="codes", align_bytes=64)
@@ -100,22 +101,22 @@ def tile_scan_pb_t_kernel(tc, query, wc, w_lin, b_lin, w_gate, b_gate, out):
         bz32 = const.tile([P, P], F32)
         bias4 = const.tile([P, 4], F32)
 
-        transpose_in(0)
-        transpose_in(1)
-        copy_in(0)
-        copy_in(1)
         nc.vector.tensor_copy(out=bz32[:], in_=bz[:])
         b_ps = ps_b.tile([P, P], F32, tag="hb")
         nc.tensor.transpose(b_ps[:], bz32[:], ident[:])
-        nc.vector.tensor_copy(out=w_grp[:], in_=w_raw[:].rearrange("p w t c -> p w c t"))
         nc.vector.tensor_copy(out=bias4[:, 0:2], in_=b_ps[:, 0:2])
         nc.vector.tensor_scalar_mul(out=bias4[:, 2:4], in0=b_ps[:, 2:4], scalar1=-1.0)
+        transpose_in(0)
+        copy_in(0, nc.scalar.copy)
+        nc.vector.tensor_copy(out=w_grp[:], in_=w_raw[:].rearrange("p w t c -> p w c t"))
+        transpose_in(1)
+        copy_in(1, nc.scalar.copy)
         nc.vector.quantize_mx(
             out=w_codes[:].bitcast(FP8X4), scales=w_sc[:], in_=w_grp[:].rearrange("p w c t -> p (w c t)")
         )
         quantise(0)
         transpose_in(2)
-        copy_in(2)
+        copy_in(2, nc.scalar.copy)
         transpose_in(3)
 
         def product(k):
@@ -145,11 +146,7 @@ def tile_scan_pb_t_kernel(tc, query, wc, w_lin, b_lin, w_gate, b_gate, out):
                 out=h_t[:, hf, :], in_=zs[0][:], func=ACT.Sigmoid, bias=bias4[:, 2 + hf : 3 + hf], scale=-1.0
             )
             nc.scalar.activation(out=u_t[:, hf, :], in_=zs[1][:], func=ACT.Tanh, bias=bias4[:, hf : hf + 1], scale=1.0)
-
-        def gate_times_update(k):
-            g, hf = divmod(k, 2)
-            h_t, u_t, w_t = st[("huw", g)]
-            nc.vector.tensor_tensor(out=w_t[:, hf, :], in0=h_t[:, hf, :], in1=u_t[:, hf, :], op=ALU.mult)
+            nc.gpsimd.tensor_tensor(out=w_t[:, hf, :], in0=h_t[:, hf, :], in1=u_t[:, hf, :], op=ALU.mult)
 
         def blend(m):
             g, s = divmod(m, 2)
@@ -171,11 +168,9 @@ def tile_scan_pb_t_kernel(tc, query, wc, w_lin, b_lin, w_gate, b_gate, out):
 
         for k in range(NH + 3):
             if k + 3 < NH:
-                copy_in(k + 3)
+                copy_in(k + 3, nc.scalar.copy)
             if k < NH:
                 product(k)
-            if 1 <= k <= NH:
-                gate_times_update(k - 1)
             if k >= 3:
                 blend(k - 3)
             if k + 4 < NH:

@@ -15,9 +15,11 @@ P = 128
 D = 256
 TOK = 8192
 JP = TOK // P
-TPG = 4
-NG = JP // TPG
-NH = 2 * NG
+TPU = 2
+UT = TPU * P
+NU = JP // TPU
+LEAD = 3
+LAG = 2
 FLOPS = 2 * TOK * 512 * 512
 
 
@@ -30,15 +32,15 @@ def tile_scan_pb_t_kernel(tc, query, wc, w_lin, b_lin, w_gate, b_gate, out):
     with ExitStack() as ctx:
         ctx.enter_context(tc.manual_schedule())
         const = ctx.enter_context(tc.tile_pool(name="const", bufs=1))
-        xpool = ctx.enter_context(tc.tile_pool(name="xpool", bufs=NG))
-        opool = ctx.enter_context(tc.tile_pool(name="opool", bufs=NH))
+        xpool = ctx.enter_context(tc.tile_pool(name="xpool", bufs=NU))
+        opool = ctx.enter_context(tc.tile_pool(name="opool", bufs=NU))
         gpool = ctx.enter_context(tc.tile_pool(name="gpool", bufs=2))
-        kpool = ctx.enter_context(tc.tile_pool(name="kpool", bufs=3))
-        apool = ctx.enter_context(tc.tile_pool(name="apool", bufs=3))
+        kpool = ctx.enter_context(tc.tile_pool(name="kpool", bufs=4))
+        apool = ctx.enter_context(tc.tile_pool(name="apool", bufs=4))
         npool = ctx.enter_context(tc.tile_pool(name="npool", bufs=2))
         ps_ct = ctx.enter_context(tc.psum_pool(name="ps_ct", bufs=1))
-        ps_z = ctx.enter_context(tc.psum_pool(name="ps_z", bufs=3))
-        ps_b = ctx.enter_context(tc.psum_pool(name="ps_b", bufs=2))
+        ps_z = ctx.enter_context(tc.psum_pool(name="ps_z", bufs=4))
+        ps_b = ctx.enter_context(tc.psum_pool(name="ps_b", bufs=3))
 
         ident = const.tile([P, P], F32)
         make_identity(nc, ident[:])
@@ -46,15 +48,14 @@ def tile_scan_pb_t_kernel(tc, query, wc, w_lin, b_lin, w_gate, b_gate, out):
         nc.vector.memset(bz[:], 0.0)
 
         xs = []
-        for g in range(NG):
-            x_t = xpool.tile([P, TPG, 2, 2, P], BF16, tag="x")
+        for a in range(NU):
+            x_t = xpool.tile([P, TPU, 2, 2, P], BF16, tag="x")
             xs.append(x_t)
 
-        def load_x(g):
-            for s in range(2):
-                js = slice(g * TPG + 2 * s, g * TPG + 2 * s + 2)
-                nc.sync.dma_start(out=xs[g][:, 2 * s : 2 * s + 2, :, 0, :], in_=q_v[:, js, :, :])
-                nc.sync.dma_start(out=xs[g][:, 2 * s : 2 * s + 2, :, 1, :], in_=c_v[:, js, :, :])
+        def load_x(a):
+            js = slice(a * TPU, (a + 1) * TPU)
+            nc.sync.dma_start(out=xs[a][:, :, :, 0, :], in_=q_v[:, js, :, :])
+            nc.sync.dma_start(out=xs[a][:, :, :, 1, :], in_=c_v[:, js, :, :])
 
         load_x(0)
         nc.scalar.dma_start(out=bz[0:2, :], in_=b_lin.rearrange("(r c) -> r c", r=2))
@@ -66,34 +67,30 @@ def tile_scan_pb_t_kernel(tc, query, wc, w_lin, b_lin, w_gate, b_gate, out):
                 nc.scalar.dma_start(
                     out=w_raw[64 * s : 64 * s + 64, i].rearrange("m (u e) c -> m u (e c)", u=2), in_=w_v[s]
                 )
-        for g in range(1, NG):
-            load_x(g)
+        for a in range(1, NU):
+            load_x(a)
 
         st = {}
 
         def transpose_in(a):
-            g, s = divmod(a, 2)
-            x32 = xs[g][:].bitcast(F32).rearrange("p j u s w -> p j u (s w)")
-            ct = ps_ct.tile([P, 2, 2, P], F32, tag="ct")
-            for t in range(2):
+            x32 = xs[a][:].bitcast(F32).rearrange("p t u s w -> p t u (s w)")
+            ct = ps_ct.tile([P, TPU, 2, P], F32, tag="ct")
+            for t in range(TPU):
                 for u in range(2):
-                    nc.tensor.transpose(ct[:, t, u, :], x32[:, 2 * s + t, u, :], ident[:])
+                    nc.tensor.transpose(ct[:, t, u, :], x32[:, t, u, :], ident[:])
             st[("ct", a)] = ct
 
-        def copy_in(a, eng_copy):
-            g, s = divmod(a, 2)
-            if s == 0:
-                gr = gpool.tile([P, TPG * P * 4], BF16, tag="gr", align_bytes=64)
-                st[("gr", g)] = gr
-            g32 = st[("gr", g)][:].bitcast(F32)
-            dst = g32[:, s * 512 : (s + 1) * 512].rearrange("p (t n u) -> p t n u", t=2, u=2)
-            eng_copy(out=dst, in_=st[("ct", a)][:].rearrange("p t u n -> p t n u"))
+        def copy_in(a):
+            gr = gpool.tile([P, UT * 4], BF16, tag="gr", align_bytes=64)
+            dst = gr[:].bitcast(F32).rearrange("p (t n u) -> p t n u", t=TPU, u=2)
+            nc.scalar.copy(out=dst, in_=st[("ct", a)][:].rearrange("p t u n -> p t n u"))
+            st[("gr", a)] = gr
 
-        def quantise(g):
-            codes = kpool.tile([P, TPG * P], U32, tag="codes", align_bytes=64)
-            sc = kpool.tile([P, TPG * P], U8, tag="sc", align_bytes=64)
-            nc.vector.quantize_mx(out=codes[:].bitcast(FP8X4), scales=sc[:], in_=st[("gr", g)][:])
-            st[("k", g)] = (codes, sc)
+        def quantise(a):
+            codes = kpool.tile([P, UT], U32, tag="codes", align_bytes=64)
+            sc = kpool.tile([P, UT], U8, tag="sc", align_bytes=64)
+            nc.vector.quantize_mx(out=codes[:].bitcast(FP8X4), scales=sc[:], in_=st[("gr", a)][:])
+            st[("k", a)] = (codes, sc)
 
         w_grp = const.tile([P, 2, D, 4], BF16, align_bytes=64)
         w_codes = const.tile([P, 2 * D], U32, align_bytes=64)
@@ -102,35 +99,31 @@ def tile_scan_pb_t_kernel(tc, query, wc, w_lin, b_lin, w_gate, b_gate, out):
         bias4 = const.tile([P, 4], F32)
 
         nc.vector.tensor_copy(out=bz32[:], in_=bz[:])
-        b_ps = ps_b.tile([P, P], F32, tag="hb")
+        b_ps = ps_b.tile([P, P], F32, tag="bk")
         nc.tensor.transpose(b_ps[:], bz32[:], ident[:])
         nc.vector.tensor_copy(out=bias4[:, 0:2], in_=b_ps[:, 0:2])
         nc.vector.tensor_scalar_mul(out=bias4[:, 2:4], in0=b_ps[:, 2:4], scalar1=-1.0)
         transpose_in(0)
-        copy_in(0, nc.scalar.copy)
+        copy_in(0)
         nc.vector.tensor_copy(out=w_grp[:], in_=w_raw[:].rearrange("p w t c -> p w c t"))
         transpose_in(1)
-        copy_in(1, nc.scalar.copy)
+        copy_in(1)
         nc.vector.quantize_mx(
             out=w_codes[:].bitcast(FP8X4), scales=w_sc[:], in_=w_grp[:].rearrange("p w c t -> p (w c t)")
         )
         quantise(0)
+        quantise(1)
         transpose_in(2)
-        copy_in(2, nc.scalar.copy)
-        transpose_in(3)
 
-        def product(k):
-            g, hf = divmod(k, 2)
-            codes, sc = st[("k", g)]
-            if hf == 0:
-                h_t = apool.tile([P, 2, 512], F32, tag="hT")
-                u_t = apool.tile([P, 2, 512], F32, tag="uT")
-                w_t = apool.tile([P, 2, 512], F32, tag="wT")
-                st[("huw", g)] = (h_t, u_t, w_t)
-            h_t, u_t, w_t = st[("huw", g)]
+        def product(a):
+            codes, sc = st[("k", a)]
+            h_t = apool.tile([P, 2, UT], F32, tag="hT")
+            u_t = apool.tile([P, 2, UT], F32, tag="uT")
+            w_t = apool.tile([P, 2, UT], F32, tag="wT")
+            st[("hw", a)] = (h_t, w_t)
             zs = []
-            for c in (2 + hf, hf):
-                z = ps_z.tile([P, 512], F32, tag="z")
+            for c in (2, 0, 3, 1):
+                z = ps_z.tile([P, UT], F32, tag="z")
                 cs = slice(c * P, (c + 1) * P)
                 nc.tensor.matmul_mx(
                     out=z[:],
@@ -142,38 +135,51 @@ def tile_scan_pb_t_kernel(tc, query, wc, w_lin, b_lin, w_gate, b_gate, out):
                     stop=True,
                 )
                 zs.append(z)
-            nc.scalar.activation(
-                out=h_t[:, hf, :], in_=zs[0][:], func=ACT.Sigmoid, bias=bias4[:, 2 + hf : 3 + hf], scale=-1.0
-            )
-            nc.scalar.activation(out=u_t[:, hf, :], in_=zs[1][:], func=ACT.Tanh, bias=bias4[:, hf : hf + 1], scale=1.0)
-            nc.gpsimd.tensor_tensor(out=w_t[:, hf, :], in0=h_t[:, hf, :], in1=u_t[:, hf, :], op=ALU.mult)
+            for hf in range(2):
+                nc.scalar.activation(
+                    out=h_t[:, hf, :], in_=zs[2 * hf][:], func=ACT.Sigmoid, bias=bias4[:, 2 + hf : 3 + hf], scale=-1.0
+                )
+                nc.scalar.activation(
+                    out=u_t[:, hf, :], in_=zs[2 * hf + 1][:], func=ACT.Tanh, bias=bias4[:, hf : hf + 1], scale=1.0
+                )
+            nc.gpsimd.tensor_tensor(out=w_t[:], in0=h_t[:], in1=u_t[:], op=ALU.mult)
 
-        def blend(m):
-            g, s = divmod(m, 2)
-            h_t, u_t, w_t = st[("huw", g)]
-            hb = ps_b.tile([P, 4, P], F32, tag="hb")
-            wb = ps_b.tile([P, 4, P], F32, tag="wb")
-            for (dst, src) in ((hb, h_t), (wb, w_t)):
-                for t in range(2):
+        def transpose_back(a):
+            banks = []
+            for src in st[("hw", a)]:
+                bk = ps_b.tile([P, 2 * TPU, P], F32, tag="bk")
+                for t in range(TPU):
                     for hf in range(2):
-                        t0 = (2 * s + t) * P
-                        nc.tensor.transpose(dst[:, 2 * t + hf, :], src[:, hf, t0 : t0 + P], ident[:])
-            q_nat = xs[g][:].rearrange("p j u s c -> p (j u) s c")[:, 4 * s : 4 * s + 4, 0, :]
-            na = npool.tile([P, 4, P], F32, tag="na")
-            nc.vector.scalar_tensor_tensor(out=na[:], in0=hb[:], scalar=-1.0, in1=q_nat, op0=ALU.add, op1=ALU.mult)
-            o_t = opool.tile([P, 4, P], F32, tag="o")
-            nc.vector.tensor_tensor(out=o_t[:], in0=wb[:], in1=na[:], op=ALU.subtract)
-            j0 = g * TPG + 2 * s
-            nc.sync.dma_start(out=o_v[:, j0 : j0 + 2, :], in_=o_t[:].rearrange("p (t hf) c -> p t (hf c)", t=2))
+                        nc.tensor.transpose(bk[:, 2 * t + hf, :], src[:, hf, t * P : (t + 1) * P], ident[:])
+                banks.append(bk)
+            st[("bk", a)] = banks
 
-        for k in range(NH + 3):
-            if k + 3 < NH:
-                copy_in(k + 3, nc.scalar.copy)
-            if k < NH:
+        def blend_first(a):
+            hb = st[("bk", a)][0]
+            q_nat = xs[a][:].rearrange("p t u s c -> p (t u) s c")[:, :, 0, :]
+            na = npool.tile([P, 2 * TPU, P], F32, tag="na")
+            nc.vector.scalar_tensor_tensor(out=na[:], in0=hb[:], scalar=-1.0, in1=q_nat, op0=ALU.add, op1=ALU.mult)
+            st[("na", a)] = na
+
+        def blend_second(a):
+            wb = st[("bk", a)][1]
+            o_t = opool.tile([P, 2 * TPU, P], F32, tag="o")
+            nc.vector.tensor_tensor(out=o_t[:], in0=wb[:], in1=st[("na", a)][:], op=ALU.subtract)
+            nc.sync.dma_start(
+                out=o_v[:, a * TPU : (a + 1) * TPU, :], in_=o_t[:].rearrange("p (t hf) c -> p t (hf c)", t=TPU)
+            )
+
+        for k in range(NU + LAG):
+            if k + LEAD - 1 < NU:
+                copy_in(k + LEAD - 1)
+            if k < NU:
                 product(k)
-            if k >= 3:
-                blend(k - 3)
-            if k + 4 < NH:
-                transpose_in(k + 4)
-            if k % 2 == 0 and (k + 2) // 2 < NG:
-                quantise((k + 2) // 2)
+            if k >= LAG:
+                transpose_back(k - LAG)
+                blend_first(k - LAG)
+            if k + LEAD - 1 < NU:
+                quantise(k + LEAD - 1)
+            if k >= LAG:
+                blend_second(k - LAG)
+            if k + LEAD < NU:
+                transpose_in(k + LEAD)

@@ -13,173 +13,190 @@ ALU = mybir.AluOpType
 
 P = 128
 D = 256
-TOK = 8192
-JP = TOK // P
-TPU = 2
-UT = TPU * P
-NU = JP // TPU
+TOKENS = 8 * 8 * 128
+PER_PARTITION = TOKENS // P
+TILES = 2
+UNIT = TILES * P
+UNITS = PER_PARTITION // TILES
 LEAD = 3
 LAG = 2
-FLOPS = 2 * TOK * 512 * 512
+CHUNKS = (2, 0, 3, 1)
+FLOPS = 2 * TOKENS * 2 * D * 2 * D
 
 
 def tile_scan_pb_t_kernel(tc, query, wc, w_lin, b_lin, w_gate, b_gate, out):
     nc = tc.nc
-    q_v = query.flatten_outer_dims().rearrange("(p j) (u c) -> p j u c", j=JP, u=2)
-    c_v = wc.flatten_outer_dims().rearrange("(p j) (u c) -> p j u c", j=JP, u=2)
-    o_v = out.flatten_outer_dims().rearrange("(p j) d -> p j d", j=JP)
+    q_dram = query.flatten_outer_dims().rearrange("(p j) (u c) -> p j u c", j=PER_PARTITION, u=2)
+    c_dram = wc.flatten_outer_dims().rearrange("(p j) (u c) -> p j u c", j=PER_PARTITION, u=2)
+    o_dram = out.flatten_outer_dims().rearrange("(p j) d -> p j d", j=PER_PARTITION)
 
     with ExitStack() as ctx:
         ctx.enter_context(tc.manual_schedule())
         const = ctx.enter_context(tc.tile_pool(name="const", bufs=1))
-        xpool = ctx.enter_context(tc.tile_pool(name="xpool", bufs=NU))
-        opool = ctx.enter_context(tc.tile_pool(name="opool", bufs=NU))
-        gpool = ctx.enter_context(tc.tile_pool(name="gpool", bufs=2))
-        kpool = ctx.enter_context(tc.tile_pool(name="kpool", bufs=4))
-        apool = ctx.enter_context(tc.tile_pool(name="apool", bufs=4))
-        npool = ctx.enter_context(tc.tile_pool(name="npool", bufs=2))
-        ps_ct = ctx.enter_context(tc.psum_pool(name="ps_ct", bufs=1))
-        ps_z = ctx.enter_context(tc.psum_pool(name="ps_z", bufs=4))
-        ps_b = ctx.enter_context(tc.psum_pool(name="ps_b", bufs=3))
+        x_pool = ctx.enter_context(tc.tile_pool(name="x_pool", bufs=UNITS))
+        o_pool = ctx.enter_context(tc.tile_pool(name="o_pool", bufs=UNITS))
+        grouped_pool = ctx.enter_context(tc.tile_pool(name="grouped_pool", bufs=2))
+        packed_pool = ctx.enter_context(tc.tile_pool(name="packed_pool", bufs=LEAD + 1))
+        act_pool = ctx.enter_context(tc.tile_pool(name="act_pool", bufs=LAG + 2))
+        blend_pool = ctx.enter_context(tc.tile_pool(name="blend_pool", bufs=2))
+        in_psum = ctx.enter_context(tc.psum_pool(name="in_psum", bufs=1))
+        z_psum = ctx.enter_context(tc.psum_pool(name="z_psum", bufs=4))
+        back_psum = ctx.enter_context(tc.psum_pool(name="back_psum", bufs=3))
 
-        ident = const.tile([P, P], F32)
-        make_identity(nc, ident[:])
-        bz = const.tile([P, P], BF16)
-        nc.vector.memset(bz[:], 0.0)
+        identity = const.tile([P, P], F32)
+        make_identity(nc, identity[:])
+        bias_rows = const.tile([P, P], BF16)
+        nc.vector.memset(bias_rows[:], 0.0)
+        table_warmer = const.tile([P, 1], F32)
+        nc.vector.memset(table_warmer[:], 0.0)
 
-        xs = []
-        for a in range(NU):
-            x_t = xpool.tile([P, TPU, 2, 2, P], BF16, tag="x")
-            xs.append(x_t)
+        x_of = []
+        for a in range(UNITS):
+            x = x_pool.tile([P, TILES, 2, 2, P], BF16, tag="x")
+            x_of.append(x)
 
-        def load_x(a):
-            js = slice(a * TPU, (a + 1) * TPU)
-            nc.sync.dma_start(out=xs[a][:, :, :, 0, :], in_=q_v[:, js, :, :])
-            nc.sync.dma_start(out=xs[a][:, :, :, 1, :], in_=c_v[:, js, :, :])
+        def load_unit(a):
+            tokens = slice(a * TILES, (a + 1) * TILES)
+            nc.sync.dma_start(out=x_of[a][:, :, :, 0, :], in_=q_dram[:, tokens, :, :])
+            nc.sync.dma_start(out=x_of[a][:, :, :, 1, :], in_=c_dram[:, tokens, :, :])
 
-        load_x(0)
-        nc.scalar.dma_start(out=bz[0:2, :], in_=b_lin.rearrange("(r c) -> r c", r=2))
-        nc.scalar.dma_start(out=bz[2:4, :], in_=b_gate.rearrange("(r c) -> r c", r=2))
-        w_raw = const.tile([P, 2, 4, D], BF16)
+        load_unit(0)
+        nc.scalar.dma_start(out=bias_rows[0:2, :], in_=b_lin.rearrange("(r c) -> r c", r=2))
+        nc.scalar.dma_start(out=bias_rows[2:4, :], in_=b_gate.rearrange("(r c) -> r c", r=2))
+        w_rows = const.tile([P, 2, 4, D], BF16)
         for i, w in enumerate((w_lin, w_gate)):
-            w_v = w.rearrange("(s u m e) c -> s m u (e c)", s=2, u=2, e=2)
+            w_dram = w.rearrange("(s u m e) c -> s m u (e c)", s=2, u=2, e=2)
             for s in range(2):
                 nc.scalar.dma_start(
-                    out=w_raw[64 * s : 64 * s + 64, i].rearrange("m (u e) c -> m u (e c)", u=2), in_=w_v[s]
+                    out=w_rows[64 * s : 64 * s + 64, i].rearrange("m (u e) c -> m u (e c)", u=2), in_=w_dram[s]
                 )
-        for a in range(1, NU):
-            load_x(a)
+        nc.scalar.activation(out=table_warmer[:], in_=table_warmer[:], func=ACT.Sigmoid)
+        for a in range(1, UNITS):
+            load_unit(a)
 
-        st = {}
+        in_bank_of = {}
+        grouped_of = {}
+        packed_of = {}
+        h_w_of = {}
+        back_banks_of = {}
+        neg_gq_of = {}
 
         def transpose_in(a):
-            x32 = xs[a][:].bitcast(F32).rearrange("p t u s w -> p t u (s w)")
-            ct = ps_ct.tile([P, TPU, 2, P], F32, tag="ct")
-            for t in range(TPU):
+            words = x_of[a][:].bitcast(F32).rearrange("p t u s w -> p t u (s w)")
+            bank = in_psum.tile([P, TILES, 2, P], F32, tag="in_bank")
+            for t in range(TILES):
                 for u in range(2):
-                    nc.tensor.transpose(ct[:, t, u, :], x32[:, t, u, :], ident[:])
-            st[("ct", a)] = ct
+                    nc.tensor.transpose(bank[:, t, u, :], words[:, t, u, :], identity[:])
+            in_bank_of[a] = bank
 
         def copy_in(a):
-            gr = gpool.tile([P, UT * 4], BF16, tag="gr", align_bytes=64)
-            dst = gr[:].bitcast(F32).rearrange("p (t n u) -> p t n u", t=TPU, u=2)
-            nc.scalar.copy(out=dst, in_=st[("ct", a)][:].rearrange("p t u n -> p t n u"))
-            st[("gr", a)] = gr
+            grouped = grouped_pool.tile([P, UNIT * 4], BF16, tag="grouped", align_bytes=64)
+            nc.scalar.copy(
+                out=grouped[:].bitcast(F32).rearrange("p (t n u) -> p t n u", t=TILES, u=2),
+                in_=in_bank_of[a][:].rearrange("p t u n -> p t n u"),
+            )
+            grouped_of[a] = grouped
 
         def quantise(a):
-            codes = kpool.tile([P, UT], U32, tag="codes", align_bytes=64)
-            sc = kpool.tile([P, UT], U8, tag="sc", align_bytes=64)
-            nc.vector.quantize_mx(out=codes[:].bitcast(FP8X4), scales=sc[:], in_=st[("gr", a)][:])
-            st[("k", a)] = (codes, sc)
+            words = packed_pool.tile([P, UNIT], U32, tag="words", align_bytes=64)
+            scales = packed_pool.tile([P, UNIT], U8, tag="scales", align_bytes=64)
+            nc.vector.quantize_mx(out=words[:].bitcast(FP8X4), scales=scales[:], in_=grouped_of[a][:])
+            packed_of[a] = (words, scales)
 
-        w_grp = const.tile([P, 2, D, 4], BF16, align_bytes=64)
-        w_codes = const.tile([P, 2 * D], U32, align_bytes=64)
-        w_sc = const.tile([P, 2 * D], U8, align_bytes=64)
-        bz32 = const.tile([P, P], F32)
-        bias4 = const.tile([P, 4], F32)
+        def products(a):
+            words, scales = packed_of[a]
+            h = act_pool.tile([P, 2, UNIT], F32, tag="h")
+            u = act_pool.tile([P, 2, UNIT], F32, tag="u")
+            w = act_pool.tile([P, 2, UNIT], F32, tag="w")
+            z_of = {}
+            for chunk in CHUNKS:
+                z = z_psum.tile([P, UNIT], F32, tag="z")
+                columns = slice(chunk * P, (chunk + 1) * P)
+                nc.tensor.matmul_mx(
+                    out=z[:],
+                    lhsT=w_words[:, columns].bitcast(FP8X4),
+                    lhsT_scale=w_scales[:, columns],
+                    rhs=words[:].bitcast(FP8X4),
+                    rhs_scale=scales[:],
+                    start=True,
+                    stop=True,
+                )
+                z_of[chunk] = z
+            for half in range(2):
+                nc.scalar.activation(
+                    out=h[:, half, :], in_=z_of[2 + half][:], func=ACT.Sigmoid,
+                    bias=bias[:, 2 + half : 3 + half], scale=-1.0,
+                )
+                nc.scalar.activation(
+                    out=u[:, half, :], in_=z_of[half][:], func=ACT.Tanh, bias=bias[:, half : half + 1], scale=1.0
+                )
+            nc.gpsimd.tensor_tensor(out=w[:], in0=h[:], in1=u[:], op=ALU.mult)
+            h_w_of[a] = (h, w)
 
-        nc.vector.tensor_copy(out=bz32[:], in_=bz[:])
-        b_ps = ps_b.tile([P, P], F32, tag="bk")
-        nc.tensor.transpose(b_ps[:], bz32[:], ident[:])
-        nc.vector.tensor_copy(out=bias4[:, 0:2], in_=b_ps[:, 0:2])
-        nc.vector.tensor_scalar_mul(out=bias4[:, 2:4], in0=b_ps[:, 2:4], scalar1=-1.0)
+        def transpose_back(a):
+            banks = []
+            for source in h_w_of[a]:
+                bank = back_psum.tile([P, 2 * TILES, P], F32, tag="back_bank")
+                for t in range(TILES):
+                    for half in range(2):
+                        nc.tensor.transpose(
+                            bank[:, 2 * t + half, :], source[:, half, t * P : (t + 1) * P], identity[:]
+                        )
+                banks.append(bank)
+            back_banks_of[a] = banks
+
+        def blend_query(a):
+            h_bank = back_banks_of[a][0]
+            q = x_of[a][:].rearrange("p t u s c -> p (t u) s c")[:, :, 0, :]
+            neg_gq = blend_pool.tile([P, 2 * TILES, P], F32, tag="neg_gq")
+            nc.vector.scalar_tensor_tensor(
+                out=neg_gq[:], in0=h_bank[:], scalar=-1.0, in1=q, op0=ALU.add, op1=ALU.mult
+            )
+            neg_gq_of[a] = neg_gq
+
+        def blend_update_and_store(a):
+            w_bank = back_banks_of[a][1]
+            o = o_pool.tile([P, 2 * TILES, P], F32, tag="o")
+            nc.vector.tensor_tensor(out=o[:], in0=w_bank[:], in1=neg_gq_of[a][:], op=ALU.subtract)
+            nc.sync.dma_start(
+                out=o_dram[:, a * TILES : (a + 1) * TILES, :],
+                in_=o[:].rearrange("p (t half) c -> p t (half c)", t=TILES),
+            )
+
+        w_grouped = const.tile([P, 2, D, 4], BF16, align_bytes=64)
+        w_words = const.tile([P, 2 * D], U32, align_bytes=64)
+        w_scales = const.tile([P, 2 * D], U8, align_bytes=64)
+        bias_rows_f32 = const.tile([P, P], F32)
+        bias = const.tile([P, 4], F32)
+
+        nc.vector.tensor_copy(out=bias_rows_f32[:], in_=bias_rows[:])
+        bias_bank = back_psum.tile([P, P], F32, tag="back_bank")
+        nc.tensor.transpose(bias_bank[:], bias_rows_f32[:], identity[:])
+        nc.vector.tensor_copy(out=bias[:, 0:2], in_=bias_bank[:, 0:2])
+        nc.vector.tensor_scalar_mul(out=bias[:, 2:4], in0=bias_bank[:, 2:4], scalar1=-1.0)
         transpose_in(0)
         copy_in(0)
-        nc.vector.tensor_copy(out=w_grp[:], in_=w_raw[:].rearrange("p w t c -> p w c t"))
+        nc.vector.tensor_copy(out=w_grouped[:], in_=w_rows[:].rearrange("p i t c -> p i c t"))
         transpose_in(1)
         copy_in(1)
         nc.vector.quantize_mx(
-            out=w_codes[:].bitcast(FP8X4), scales=w_sc[:], in_=w_grp[:].rearrange("p w c t -> p (w c t)")
+            out=w_words[:].bitcast(FP8X4), scales=w_scales[:], in_=w_grouped[:].rearrange("p i c t -> p (i c t)")
         )
         quantise(0)
         quantise(1)
         transpose_in(2)
 
-        def product(a):
-            codes, sc = st[("k", a)]
-            h_t = apool.tile([P, 2, UT], F32, tag="hT")
-            u_t = apool.tile([P, 2, UT], F32, tag="uT")
-            w_t = apool.tile([P, 2, UT], F32, tag="wT")
-            st[("hw", a)] = (h_t, w_t)
-            zs = []
-            for c in (2, 0, 3, 1):
-                z = ps_z.tile([P, UT], F32, tag="z")
-                cs = slice(c * P, (c + 1) * P)
-                nc.tensor.matmul_mx(
-                    out=z[:],
-                    lhsT=w_codes[:, cs].bitcast(FP8X4),
-                    lhsT_scale=w_sc[:, cs],
-                    rhs=codes[:].bitcast(FP8X4),
-                    rhs_scale=sc[:],
-                    start=True,
-                    stop=True,
-                )
-                zs.append(z)
-            for hf in range(2):
-                nc.scalar.activation(
-                    out=h_t[:, hf, :], in_=zs[2 * hf][:], func=ACT.Sigmoid, bias=bias4[:, 2 + hf : 3 + hf], scale=-1.0
-                )
-                nc.scalar.activation(
-                    out=u_t[:, hf, :], in_=zs[2 * hf + 1][:], func=ACT.Tanh, bias=bias4[:, hf : hf + 1], scale=1.0
-                )
-            nc.gpsimd.tensor_tensor(out=w_t[:], in0=h_t[:], in1=u_t[:], op=ALU.mult)
-
-        def transpose_back(a):
-            banks = []
-            for src in st[("hw", a)]:
-                bk = ps_b.tile([P, 2 * TPU, P], F32, tag="bk")
-                for t in range(TPU):
-                    for hf in range(2):
-                        nc.tensor.transpose(bk[:, 2 * t + hf, :], src[:, hf, t * P : (t + 1) * P], ident[:])
-                banks.append(bk)
-            st[("bk", a)] = banks
-
-        def blend_first(a):
-            hb = st[("bk", a)][0]
-            q_nat = xs[a][:].rearrange("p t u s c -> p (t u) s c")[:, :, 0, :]
-            na = npool.tile([P, 2 * TPU, P], F32, tag="na")
-            nc.vector.scalar_tensor_tensor(out=na[:], in0=hb[:], scalar=-1.0, in1=q_nat, op0=ALU.add, op1=ALU.mult)
-            st[("na", a)] = na
-
-        def blend_second(a):
-            wb = st[("bk", a)][1]
-            o_t = opool.tile([P, 2 * TPU, P], F32, tag="o")
-            nc.vector.tensor_tensor(out=o_t[:], in0=wb[:], in1=st[("na", a)][:], op=ALU.subtract)
-            nc.sync.dma_start(
-                out=o_v[:, a * TPU : (a + 1) * TPU, :], in_=o_t[:].rearrange("p (t hf) c -> p t (hf c)", t=TPU)
-            )
-
-        for k in range(NU + LAG):
-            if k + LEAD - 1 < NU:
-                copy_in(k + LEAD - 1)
-            if k < NU:
-                product(k)
-            if k >= LAG:
-                transpose_back(k - LAG)
-                blend_first(k - LAG)
-            if k + LEAD - 1 < NU:
-                quantise(k + LEAD - 1)
-            if k >= LAG:
-                blend_second(k - LAG)
-            if k + LEAD < NU:
-                transpose_in(k + LEAD)
+        for a in range(UNITS + LAG):
+            if a + LEAD - 1 < UNITS:
+                copy_in(a + LEAD - 1)
+            if a < UNITS:
+                products(a)
+            if a >= LAG:
+                transpose_back(a - LAG)
+                blend_query(a - LAG)
+            if a + LEAD - 1 < UNITS:
+                quantise(a + LEAD - 1)
+            if a >= LAG:
+                blend_update_and_store(a - LAG)
+            if a + LEAD < UNITS:
+                transpose_in(a + LEAD)

@@ -26,8 +26,8 @@ FLOPS = 2 * TOKENS * 2 * D * 2 * D
 
 def tile_scan_pb_t_kernel(tc, query, wc, w_lin, b_lin, w_gate, b_gate, out):
     nc = tc.nc
-    q_dram = query.flatten_outer_dims().rearrange("(p j) (u c) -> p j u c", j=PER_PARTITION, u=2)
-    c_dram = wc.flatten_outer_dims().rearrange("(p j) (u c) -> p j u c", j=PER_PARTITION, u=2)
+    q_dram = query.flatten_outer_dims().rearrange("(p j) (f c) -> p j f c", j=PER_PARTITION, f=2)
+    c_dram = wc.flatten_outer_dims().rearrange("(p j) (f c) -> p j f c", j=PER_PARTITION, f=2)
     o_dram = out.flatten_outer_dims().rearrange("(p j) d -> p j d", j=PER_PARTITION)
 
     with ExitStack() as ctx:
@@ -47,8 +47,6 @@ def tile_scan_pb_t_kernel(tc, query, wc, w_lin, b_lin, w_gate, b_gate, out):
         make_identity(nc, identity[:])
         bias_rows = const.tile([P, P], BF16)
         nc.vector.memset(bias_rows[:], 0.0)
-        table_warmer = const.tile([P, 1], F32)
-        nc.vector.memset(table_warmer[:], 0.0)
 
         x_of = []
         for a in range(UNITS):
@@ -64,36 +62,35 @@ def tile_scan_pb_t_kernel(tc, query, wc, w_lin, b_lin, w_gate, b_gate, out):
         nc.scalar.dma_start(out=bias_rows[0:2, :], in_=b_lin.rearrange("(r c) -> r c", r=2))
         nc.scalar.dma_start(out=bias_rows[2:4, :], in_=b_gate.rearrange("(r c) -> r c", r=2))
         w_rows = const.tile([P, 2, 4, D], BF16)
-        for i, w in enumerate((w_lin, w_gate)):
-            w_dram = w.rearrange("(s u m e) c -> s m u (e c)", s=2, u=2, e=2)
+        for i, weight in enumerate((w_lin, w_gate)):
+            w_dram = weight.rearrange("(s f m e) o -> s m f (e o)", s=2, f=2, e=2)
             for s in range(2):
                 nc.scalar.dma_start(
-                    out=w_rows[64 * s : 64 * s + 64, i].rearrange("m (u e) c -> m u (e c)", u=2), in_=w_dram[s]
+                    out=w_rows[64 * s : 64 * s + 64, i].rearrange("m (f e) o -> m f (e o)", f=2), in_=w_dram[s]
                 )
-        nc.scalar.activation(out=table_warmer[:], in_=table_warmer[:], func=ACT.Sigmoid)
         for a in range(1, UNITS):
             load_unit(a)
 
         in_bank_of = {}
         grouped_of = {}
         packed_of = {}
-        h_w_of = {}
+        h_and_h_upd_of = {}
         back_banks_of = {}
         neg_gq_of = {}
 
         def transpose_in(a):
-            words = x_of[a][:].bitcast(F32).rearrange("p t u s w -> p t u (s w)")
-            bank = in_psum.tile([P, TILES, 2, P], F32, tag="in_bank")
+            pairs = x_of[a][:].bitcast(F32).rearrange("p t f s w -> p t f (s w)")
+            in_bank = in_psum.tile([P, TILES, 2, P], F32, tag="in_bank")
             for t in range(TILES):
-                for u in range(2):
-                    nc.tensor.transpose(bank[:, t, u, :], words[:, t, u, :], identity[:])
-            in_bank_of[a] = bank
+                for f in range(2):
+                    nc.tensor.transpose(in_bank[:, t, f, :], pairs[:, t, f, :], identity[:])
+            in_bank_of[a] = in_bank
 
         def copy_in(a):
             grouped = grouped_pool.tile([P, UNIT * 4], BF16, tag="grouped", align_bytes=64)
             nc.scalar.copy(
-                out=grouped[:].bitcast(F32).rearrange("p (t n u) -> p t n u", t=TILES, u=2),
-                in_=in_bank_of[a][:].rearrange("p t u n -> p t n u"),
+                out=grouped[:].bitcast(F32).rearrange("p (t n f) -> p t n f", t=TILES, f=2),
+                in_=in_bank_of[a][:].rearrange("p t f n -> p t n f"),
             )
             grouped_of[a] = grouped
 
@@ -106,8 +103,8 @@ def tile_scan_pb_t_kernel(tc, query, wc, w_lin, b_lin, w_gate, b_gate, out):
         def products(a):
             words, scales = packed_of[a]
             h = act_pool.tile([P, 2, UNIT], F32, tag="h")
-            u = act_pool.tile([P, 2, UNIT], F32, tag="u")
-            w = act_pool.tile([P, 2, UNIT], F32, tag="w")
+            upd = act_pool.tile([P, 2, UNIT], F32, tag="upd")
+            h_upd = act_pool.tile([P, 2, UNIT], F32, tag="h_upd")
             z_of = {}
             for chunk in CHUNKS:
                 z = z_psum.tile([P, UNIT], F32, tag="z")
@@ -122,32 +119,31 @@ def tile_scan_pb_t_kernel(tc, query, wc, w_lin, b_lin, w_gate, b_gate, out):
                     stop=True,
                 )
                 z_of[chunk] = z
-            for half in range(2):
+            for f in range(2):
                 nc.scalar.activation(
-                    out=h[:, half, :], in_=z_of[2 + half][:], func=ACT.Sigmoid,
-                    bias=bias[:, 2 + half : 3 + half], scale=-1.0,
+                    out=h[:, f, :], in_=z_of[2 + f][:], func=ACT.Sigmoid, bias=bias[:, 2 + f : 3 + f], scale=-1.0
                 )
                 nc.scalar.activation(
-                    out=u[:, half, :], in_=z_of[half][:], func=ACT.Tanh, bias=bias[:, half : half + 1], scale=1.0
+                    out=upd[:, f, :], in_=z_of[f][:], func=ACT.Tanh, bias=bias[:, f : f + 1], scale=1.0
                 )
-            nc.gpsimd.tensor_tensor(out=w[:], in0=h[:], in1=u[:], op=ALU.mult)
-            h_w_of[a] = (h, w)
+            nc.gpsimd.tensor_tensor(out=h_upd[:], in0=h[:], in1=upd[:], op=ALU.mult)
+            h_and_h_upd_of[a] = (h, h_upd)
 
         def transpose_back(a):
             banks = []
-            for source in h_w_of[a]:
-                bank = back_psum.tile([P, 2 * TILES, P], F32, tag="back_bank")
+            for source in h_and_h_upd_of[a]:
+                back_bank = back_psum.tile([P, 2 * TILES, P], F32, tag="back_bank")
                 for t in range(TILES):
-                    for half in range(2):
+                    for f in range(2):
                         nc.tensor.transpose(
-                            bank[:, 2 * t + half, :], source[:, half, t * P : (t + 1) * P], identity[:]
+                            back_bank[:, 2 * t + f, :], source[:, f, t * P : (t + 1) * P], identity[:]
                         )
-                banks.append(bank)
+                banks.append(back_bank)
             back_banks_of[a] = banks
 
         def blend_query(a):
             h_bank = back_banks_of[a][0]
-            q = x_of[a][:].rearrange("p t u s c -> p (t u) s c")[:, :, 0, :]
+            q = x_of[a][:].rearrange("p t f s c -> p (t f) s c")[:, :, 0, :]
             neg_gq = blend_pool.tile([P, 2 * TILES, P], F32, tag="neg_gq")
             nc.vector.scalar_tensor_tensor(
                 out=neg_gq[:], in0=h_bank[:], scalar=-1.0, in1=q, op0=ALU.add, op1=ALU.mult
@@ -155,12 +151,11 @@ def tile_scan_pb_t_kernel(tc, query, wc, w_lin, b_lin, w_gate, b_gate, out):
             neg_gq_of[a] = neg_gq
 
         def blend_update_and_store(a):
-            w_bank = back_banks_of[a][1]
+            h_upd_bank = back_banks_of[a][1]
             o = o_pool.tile([P, 2 * TILES, P], F32, tag="o")
-            nc.vector.tensor_tensor(out=o[:], in0=w_bank[:], in1=neg_gq_of[a][:], op=ALU.subtract)
+            nc.vector.tensor_tensor(out=o[:], in0=h_upd_bank[:], in1=neg_gq_of[a][:], op=ALU.subtract)
             nc.sync.dma_start(
-                out=o_dram[:, a * TILES : (a + 1) * TILES, :],
-                in_=o[:].rearrange("p (t half) c -> p t (half c)", t=TILES),
+                out=o_dram[:, a * TILES : (a + 1) * TILES, :], in_=o[:].rearrange("p (t f) c -> p t (f c)", t=TILES)
             )
 
         w_grouped = const.tile([P, 2, D, 4], BF16, align_bytes=64)
@@ -176,11 +171,11 @@ def tile_scan_pb_t_kernel(tc, query, wc, w_lin, b_lin, w_gate, b_gate, out):
         nc.vector.tensor_scalar_mul(out=bias[:, 2:4], in0=bias_bank[:, 2:4], scalar1=-1.0)
         transpose_in(0)
         copy_in(0)
-        nc.vector.tensor_copy(out=w_grouped[:], in_=w_rows[:].rearrange("p i t c -> p i c t"))
+        nc.vector.tensor_copy(out=w_grouped[:], in_=w_rows[:].rearrange("p i v o -> p i o v"))
         transpose_in(1)
         copy_in(1)
         nc.vector.quantize_mx(
-            out=w_words[:].bitcast(FP8X4), scales=w_scales[:], in_=w_grouped[:].rearrange("p i c t -> p (i c t)")
+            out=w_words[:].bitcast(FP8X4), scales=w_scales[:], in_=w_grouped[:].rearrange("p i o v -> p (i o v)")
         )
         quantise(0)
         quantise(1)

@@ -17,10 +17,8 @@ TOKENS = 8 * 8 * 128
 PER_PARTITION = TOKENS // P
 TILES = 2
 UNIT = TILES * P
-UNITS = PER_PARTITION // TILES
-LEAD = 3
-LAG = 2
-CHUNKS = (2, 0, 3, 1)
+GROUPS = ((0,),) + tuple((u, u + 1) for u in range(1, 31, 2)) + ((31,),)
+LEAD = 2
 FLOPS = 2 * TOKENS * 2 * D * 2 * D
 
 
@@ -33,23 +31,23 @@ def tile_scan_pb_t_kernel(tc, query, wc, w_lin, b_lin, w_gate, b_gate, out):
     with ExitStack() as ctx:
         ctx.enter_context(tc.manual_schedule())
         const = ctx.enter_context(tc.tile_pool(name="const", bufs=1))
-        x_pool = ctx.enter_context(tc.tile_pool(name="x_pool", bufs=UNITS))
-        o_pool = ctx.enter_context(tc.tile_pool(name="o_pool", bufs=UNITS))
-        grouped_pool = ctx.enter_context(tc.tile_pool(name="grouped_pool", bufs=2))
-        packed_pool = ctx.enter_context(tc.tile_pool(name="packed_pool", bufs=LEAD + 1))
-        act_pool = ctx.enter_context(tc.tile_pool(name="act_pool", bufs=LAG + 2))
-        blend_pool = ctx.enter_context(tc.tile_pool(name="blend_pool", bufs=2))
-        in_psum = ctx.enter_context(tc.psum_pool(name="in_psum", bufs=1))
-        z_psum = ctx.enter_context(tc.psum_pool(name="z_psum", bufs=4))
-        back_psum = ctx.enter_context(tc.psum_pool(name="back_psum", bufs=3))
+        units = PER_PARTITION // TILES
+        x_pool = ctx.enter_context(tc.tile_pool(name="x_pool", bufs=units))
+        o_pool = ctx.enter_context(tc.tile_pool(name="o_pool", bufs=units))
+        grouped_pool = ctx.enter_context(tc.tile_pool(name="grouped_pool", bufs=3))
+        packed_pool = ctx.enter_context(tc.tile_pool(name="packed_pool", bufs=LEAD + 2))
+        act_pool = ctx.enter_context(tc.tile_pool(name="act_pool", bufs=3))
+        psum = ctx.enter_context(tc.psum_pool(name="psum", bufs=8))
 
         identity = const.tile([P, P], F32)
         make_identity(nc, identity[:])
+        identity_bf16 = const.tile([P, P], BF16)
+        make_identity(nc, identity_bf16[:])
         bias_rows = const.tile([P, P], BF16)
         nc.vector.memset(bias_rows[:], 0.0)
 
         x_of = []
-        for a in range(UNITS):
+        for a in range(units):
             x = x_pool.tile([P, TILES, 2, 2, P], BF16, tag="x")
             x_of.append(x)
 
@@ -68,19 +66,20 @@ def tile_scan_pb_t_kernel(tc, query, wc, w_lin, b_lin, w_gate, b_gate, out):
                 nc.scalar.dma_start(
                     out=w_rows[64 * s : 64 * s + 64, i].rearrange("m (f e) o -> m f (e o)", f=2), in_=w_dram[s]
                 )
-        for a in range(1, UNITS):
+        for a in range(1, units):
             load_unit(a)
 
         in_bank_of = {}
         grouped_of = {}
         packed_of = {}
-        h_and_h_upd_of = {}
-        back_banks_of = {}
-        neg_gq_of = {}
+        z_of = {}
+        acts_of = {}
+        back_bank_of = {}
+        query_bank_of = {}
 
         def transpose_in(a):
             pairs = x_of[a][:].bitcast(F32).rearrange("p t f s w -> p t f (s w)")
-            in_bank = in_psum.tile([P, TILES, 2, P], F32, tag="in_bank")
+            in_bank = psum.tile([P, TILES, 2, P], F32, tag="bank")
             for t in range(TILES):
                 for f in range(2):
                     nc.tensor.transpose(in_bank[:, t, f, :], pairs[:, t, f, :], identity[:])
@@ -94,23 +93,26 @@ def tile_scan_pb_t_kernel(tc, query, wc, w_lin, b_lin, w_gate, b_gate, out):
             )
             grouped_of[a] = grouped
 
-        def quantise(a):
-            words = packed_pool.tile([P, UNIT], U32, tag="words", align_bytes=64)
-            scales = packed_pool.tile([P, UNIT], U8, tag="scales", align_bytes=64)
-            nc.vector.quantize_mx(out=words[:].bitcast(FP8X4), scales=scales[:], in_=grouped_of[a][:])
-            packed_of[a] = (words, scales)
+        def allocate_packed(g):
+            words = packed_pool.tile([P, len(GROUPS[g]) * UNIT], U32, tag="words", align_bytes=64)
+            scales = packed_pool.tile([P, len(GROUPS[g]) * UNIT], U8, tag="scales", align_bytes=64)
+            packed_of[g] = (words, scales)
 
-        def products(a):
-            words, scales = packed_of[a]
-            h = act_pool.tile([P, 2, UNIT], F32, tag="h")
-            upd = act_pool.tile([P, 2, UNIT], F32, tag="upd")
-            h_upd = act_pool.tile([P, 2, UNIT], F32, tag="h_upd")
-            z_of = {}
-            for chunk in CHUNKS:
-                z = z_psum.tile([P, UNIT], F32, tag="z")
+        def quantise(g, i):
+            words, scales = packed_of[g]
+            columns = slice(i * UNIT, (i + 1) * UNIT)
+            nc.vector.quantize_mx(
+                out=words[:, columns].bitcast(FP8X4), scales=scales[:, columns], in_=grouped_of[GROUPS[g][i]][:]
+            )
+
+        def passes(g):
+            words, scales = packed_of[g]
+            for chunk in (0, 2, 1, 3):
+                z_bank = psum.tile([P, 2 * UNIT], F32, tag="bank")
+                z = z_bank[:, 0 : len(GROUPS[g]) * UNIT]
                 columns = slice(chunk * P, (chunk + 1) * P)
                 nc.tensor.matmul_mx(
-                    out=z[:],
+                    out=z,
                     lhsT=w_words[:, columns].bitcast(FP8X4),
                     lhsT_scale=w_scales[:, columns],
                     rhs=words[:].bitcast(FP8X4),
@@ -118,42 +120,58 @@ def tile_scan_pb_t_kernel(tc, query, wc, w_lin, b_lin, w_gate, b_gate, out):
                     start=True,
                     stop=True,
                 )
-                z_of[chunk] = z
-            for f in range(2):
-                nc.scalar.activation(
-                    out=h[:, f, :], in_=z_of[2 + f][:], func=ACT.Sigmoid, bias=bias[:, 2 + f : 3 + f], scale=-1.0
-                )
-                nc.scalar.activation(
-                    out=upd[:, f, :], in_=z_of[f][:], func=ACT.Tanh, bias=bias[:, f : f + 1], scale=1.0
-                )
-            nc.gpsimd.tensor_tensor(out=h_upd[:], in0=h[:], in1=upd[:], op=ALU.mult)
-            h_and_h_upd_of[a] = (h, h_upd)
+                z_of[g, chunk] = z
+            h = act_pool.tile([P, 2, len(GROUPS[g]) * UNIT], F32, tag="h")
+            upd = act_pool.tile([P, 2, len(GROUPS[g]) * UNIT], F32, tag="upd")
+            diff = act_pool.tile([P, 2, len(GROUPS[g]) * UNIT], F32, tag="diff")
+            step = act_pool.tile([P, 2, len(GROUPS[g]) * UNIT], F32, tag="step")
+            acts_of[g] = (h, upd, diff, step)
 
-        def transpose_back(a):
-            banks = []
-            for source in h_and_h_upd_of[a]:
-                back_bank = back_psum.tile([P, 2 * TILES, P], F32, tag="back_bank")
+        def activate_h(g, f):
+            nc.scalar.activation(
+                out=acts_of[g][0][:, f, :],
+                in_=z_of[g, 2 + f],
+                func=ACT.Sigmoid,
+                bias=bias[:, 2 + f : 3 + f],
+                scale=-1.0,
+            )
+
+        def activate_upd(g, f):
+            nc.scalar.activation(
+                out=acts_of[g][1][:, f, :], in_=z_of[g, f], func=ACT.Tanh, bias=bias[:, f : f + 1], scale=1.0
+            )
+
+        def transpose_query(g):
+            query_bank = psum.tile([P, 2, 2 * UNIT], BF16, tag="bank")
+            for i, a in enumerate(GROUPS[g]):
                 for t in range(TILES):
                     for f in range(2):
-                        nc.tensor.transpose(
-                            back_bank[:, 2 * t + f, :], source[:, f, t * P : (t + 1) * P], identity[:]
-                        )
-                banks.append(back_bank)
-            back_banks_of[a] = banks
+                        n0 = i * UNIT + t * P
+                        nc.tensor.transpose(query_bank[:, f, n0 : n0 + P], x_of[a][:, t, f, 0, :], identity_bf16[:])
+            query_bank_of[g] = query_bank
 
-        def blend_query(a):
-            h_bank = back_banks_of[a][0]
-            q = x_of[a][:].rearrange("p t f s c -> p (t f) s c")[:, :, 0, :]
-            neg_gq = blend_pool.tile([P, 2 * TILES, P], F32, tag="neg_gq")
-            nc.vector.scalar_tensor_tensor(
-                out=neg_gq[:], in0=h_bank[:], scalar=-1.0, in1=q, op0=ALU.add, op1=ALU.mult
+        def blend(g, f):
+            h, upd, diff, step = acts_of[g]
+            n = len(GROUPS[g]) * UNIT
+            nc.vector.tensor_tensor(
+                out=diff[:, f, :], in0=upd[:, f, :], in1=query_bank_of[g][:, f, 0:n], op=ALU.subtract
             )
-            neg_gq_of[a] = neg_gq
+            nc.gpsimd.tensor_tensor(out=step[:, f, :], in0=h[:, f, :], in1=diff[:, f, :], op=ALU.mult)
 
-        def blend_update_and_store(a):
-            h_upd_bank = back_banks_of[a][1]
+        def transpose_back(g, i):
+            step = acts_of[g][3]
+            back_bank = psum.tile([P, 2 * TILES, P], F32, tag="bank")
+            for t in range(TILES):
+                for f in range(2):
+                    n0 = i * UNIT + t * P
+                    nc.tensor.transpose(back_bank[:, 2 * t + f, :], step[:, f, n0 : n0 + P], identity[:])
+            back_bank_of[g, i] = back_bank
+
+        def add_and_store(g, i):
+            a = GROUPS[g][i]
+            q = x_of[a][:].rearrange("p t f s c -> p (t f) s c")[:, :, 0, :]
             o = o_pool.tile([P, 2 * TILES, P], F32, tag="o")
-            nc.vector.tensor_tensor(out=o[:], in0=h_upd_bank[:], in1=neg_gq_of[a][:], op=ALU.subtract)
+            nc.vector.tensor_tensor(out=o[:], in0=back_bank_of[g, i][:], in1=q, op=ALU.add)
             nc.sync.dma_start(
                 out=o_dram[:, a * TILES : (a + 1) * TILES, :], in_=o[:].rearrange("p (t f) c -> p t (f c)", t=TILES)
             )
@@ -165,8 +183,8 @@ def tile_scan_pb_t_kernel(tc, query, wc, w_lin, b_lin, w_gate, b_gate, out):
         bias = const.tile([P, 4], F32)
 
         nc.vector.tensor_copy(out=bias_rows_f32[:], in_=bias_rows[:])
-        bias_bank = back_psum.tile([P, P], F32, tag="back_bank")
-        nc.tensor.transpose(bias_bank[:], bias_rows_f32[:], identity[:])
+        bias_bank = psum.tile([P, 4 * P], F32, tag="bank")
+        nc.tensor.transpose(bias_bank[:, 0:P], bias_rows_f32[:], identity[:])
         nc.vector.tensor_copy(out=bias[:, 0:2], in_=bias_bank[:, 0:2])
         nc.vector.tensor_scalar_mul(out=bias[:, 2:4], in0=bias_bank[:, 2:4], scalar1=-1.0)
         transpose_in(0)
@@ -174,24 +192,50 @@ def tile_scan_pb_t_kernel(tc, query, wc, w_lin, b_lin, w_gate, b_gate, out):
         nc.vector.tensor_copy(out=w_grouped[:], in_=w_rows[:].rearrange("p i v o -> p i o v"))
         transpose_in(1)
         copy_in(1)
+        transpose_query(0)
+        transpose_in(2)
+        copy_in(2)
         nc.vector.quantize_mx(
             out=w_words[:].bitcast(FP8X4), scales=w_scales[:], in_=w_grouped[:].rearrange("p i o v -> p (i o v)")
         )
-        quantise(0)
-        quantise(1)
-        transpose_in(2)
+        allocate_packed(0)
+        quantise(0, 0)
+        allocate_packed(1)
+        quantise(1, 0)
+        quantise(1, 1)
 
-        for a in range(UNITS + LAG):
-            if a + LEAD - 1 < UNITS:
-                copy_in(a + LEAD - 1)
-            if a < UNITS:
-                products(a)
-            if a >= LAG:
-                transpose_back(a - LAG)
-                blend_query(a - LAG)
-            if a + LEAD - 1 < UNITS:
-                quantise(a + LEAD - 1)
-            if a >= LAG:
-                blend_update_and_store(a - LAG)
-            if a + LEAD < UNITS:
-                transpose_in(a + LEAD)
+        for g in range(len(GROUPS) + 1):
+            ahead = g + LEAD if g + LEAD < len(GROUPS) else None
+            n_ahead = len(GROUPS[ahead]) if ahead else 0
+            n_back = len(GROUPS[g - 1]) if g >= 1 else 0
+            now = g < len(GROUPS)
+            if ahead:
+                allocate_packed(ahead)
+            if now:
+                passes(g)
+            if n_back:
+                transpose_back(g - 1, 0)
+            for i in range(n_ahead):
+                transpose_in(GROUPS[ahead][i])
+            if n_back > 1:
+                transpose_back(g - 1, 1)
+            if now:
+                for f in range(2):
+                    activate_upd(g, f)
+                    activate_h(g, f)
+            for i in range(n_ahead):
+                copy_in(GROUPS[ahead][i])
+            if now:
+                blend(g, 0)
+            if n_back:
+                add_and_store(g - 1, 0)
+            if now:
+                blend(g, 1)
+            if n_ahead:
+                quantise(ahead, 0)
+            if n_back > 1:
+                add_and_store(g - 1, 1)
+            if n_ahead > 1:
+                quantise(ahead, 1)
+            if g + 1 < len(GROUPS):
+                transpose_query(g + 1)

@@ -18,6 +18,7 @@ PER_PARTITION = TOKENS // P
 TILES = 2
 UNIT = TILES * P
 GROUPS = ((0,),) + tuple((u, u + 1) for u in range(1, 31, 2)) + ((31,),)
+PLAIN_TILES = 3
 LEAD = 2
 FLOPS = 2 * TOKENS * 2 * D * 2 * D
 
@@ -147,7 +148,13 @@ def tile_scan_pb_t_kernel(tc, query, wc, w_lin, b_lin, w_gate, b_gate, out):
                 for t in range(TILES):
                     for f in range(2):
                         n0 = i * UNIT + t * P
-                        nc.tensor.transpose(query_bank[:, f, n0 : n0 + P], x_of[a][:, t, f, 0, :], identity_bf16[:])
+                        rows = x_of[a][:, t, f, 0, :]
+                        if i * TILES + t < PLAIN_TILES:
+                            nc.tensor.matmul(
+                                query_bank[:, f, n0 : n0 + P], lhsT=rows, rhs=identity_bf16[:], start=True, stop=True
+                            )
+                        else:
+                            nc.tensor.transpose(query_bank[:, f, n0 : n0 + P], rows, identity_bf16[:])
             query_bank_of[g] = query_bank
 
         def blend(g, f):
@@ -192,7 +199,6 @@ def tile_scan_pb_t_kernel(tc, query, wc, w_lin, b_lin, w_gate, b_gate, out):
         nc.vector.tensor_copy(out=w_grouped[:], in_=w_rows[:].rearrange("p i v o -> p i o v"))
         transpose_in(1)
         copy_in(1)
-        transpose_query(0)
         transpose_in(2)
         copy_in(2)
         nc.vector.quantize_mx(
@@ -213,12 +219,11 @@ def tile_scan_pb_t_kernel(tc, query, wc, w_lin, b_lin, w_gate, b_gate, out):
                 allocate_packed(ahead)
             if now:
                 passes(g)
-            if n_back:
-                transpose_back(g - 1, 0)
+                transpose_query(g)
             for i in range(n_ahead):
                 transpose_in(GROUPS[ahead][i])
-            if n_back > 1:
-                transpose_back(g - 1, 1)
+            for i in range(n_back):
+                transpose_back(g - 1, i)
             if now:
                 for f in range(2):
                     activate_upd(g, f)
@@ -227,15 +232,12 @@ def tile_scan_pb_t_kernel(tc, query, wc, w_lin, b_lin, w_gate, b_gate, out):
                 copy_in(GROUPS[ahead][i])
             if now:
                 blend(g, 0)
+                blend(g, 1)
             if n_back:
                 add_and_store(g - 1, 0)
-            if now:
-                blend(g, 1)
             if n_ahead:
                 quantise(ahead, 0)
             if n_back > 1:
                 add_and_store(g - 1, 1)
             if n_ahead > 1:
                 quantise(ahead, 1)
-            if g + 1 < len(GROUPS):
-                transpose_query(g + 1)

@@ -86,25 +86,22 @@ def tile_scan_pb_t_kernel(tc, query, wc, w_lin, b_lin, w_gate, b_gate, out):
                     nc.tensor.transpose(in_bank[:, t, f, :], pairs[:, t, f, :], identity[:])
             in_bank_of[a] = in_bank
 
-        def copy_in(a):
-            grouped = grouped_pool.tile([P, UNIT * 4], BF16, tag="grouped", align_bytes=64)
+        def copy_in(g, i):
+            if i == 0:
+                grouped_of[g] = grouped_pool.tile(
+                    [P, len(GROUPS[g]) * UNIT * 4], BF16, name="grouped", tag="grouped", align_bytes=64
+                )
+            pairs = grouped_of[g][:, i * UNIT * 4 : (i + 1) * UNIT * 4].bitcast(F32)
             nc.scalar.copy(
-                out=grouped[:].bitcast(F32).rearrange("p (t n f) -> p t n f", t=TILES, f=2),
-                in_=in_bank_of[a][:].rearrange("p t f n -> p t n f"),
+                out=pairs.rearrange("p (t n f) -> p t n f", t=TILES, f=2),
+                in_=in_bank_of[GROUPS[g][i]][:].rearrange("p t f n -> p t n f"),
             )
-            grouped_of[a] = grouped
 
-        def allocate_packed(g):
+        def quantise(g):
             words = packed_pool.tile([P, len(GROUPS[g]) * UNIT], U32, tag="words", align_bytes=64)
             scales = packed_pool.tile([P, len(GROUPS[g]) * UNIT], U8, tag="scales", align_bytes=64)
+            nc.vector.quantize_mx(out=words[:].bitcast(FP8X4), scales=scales[:], in_=grouped_of[g][:])
             packed_of[g] = (words, scales)
-
-        def quantise(g, i):
-            words, scales = packed_of[g]
-            columns = slice(i * UNIT, (i + 1) * UNIT)
-            nc.vector.quantize_mx(
-                out=words[:, columns].bitcast(FP8X4), scales=scales[:, columns], in_=grouped_of[GROUPS[g][i]][:]
-            )
 
         def passes(g):
             words, scales = packed_of[g]
@@ -195,28 +192,23 @@ def tile_scan_pb_t_kernel(tc, query, wc, w_lin, b_lin, w_gate, b_gate, out):
         nc.vector.tensor_copy(out=bias[:, 0:2], in_=bias_bank[:, 0:2])
         nc.vector.tensor_scalar_mul(out=bias[:, 2:4], in0=bias_bank[:, 2:4], scalar1=-1.0)
         transpose_in(0)
-        copy_in(0)
+        copy_in(0, 0)
         nc.vector.tensor_copy(out=w_grouped[:], in_=w_rows[:].rearrange("p i v o -> p i o v"))
         transpose_in(1)
-        copy_in(1)
+        copy_in(1, 0)
         transpose_in(2)
-        copy_in(2)
+        copy_in(1, 1)
         nc.vector.quantize_mx(
             out=w_words[:].bitcast(FP8X4), scales=w_scales[:], in_=w_grouped[:].rearrange("p i o v -> p (i o v)")
         )
-        allocate_packed(0)
-        quantise(0, 0)
-        allocate_packed(1)
-        quantise(1, 0)
-        quantise(1, 1)
+        quantise(0)
+        quantise(1)
 
         for g in range(len(GROUPS) + 1):
             ahead = g + LEAD if g + LEAD < len(GROUPS) else None
             n_ahead = len(GROUPS[ahead]) if ahead else 0
             n_back = len(GROUPS[g - 1]) if g >= 1 else 0
             now = g < len(GROUPS)
-            if ahead:
-                allocate_packed(ahead)
             if now:
                 passes(g)
                 transpose_query(g)
@@ -229,15 +221,12 @@ def tile_scan_pb_t_kernel(tc, query, wc, w_lin, b_lin, w_gate, b_gate, out):
                     activate_upd(g, f)
                     activate_h(g, f)
             for i in range(n_ahead):
-                copy_in(GROUPS[ahead][i])
+                copy_in(ahead, i)
             if now:
                 blend(g, 0)
+            if 1 <= g < len(GROUPS) - 1:
+                quantise(g + 1)
+            if now:
                 blend(g, 1)
-            if n_back:
-                add_and_store(g - 1, 0)
-            if n_ahead:
-                quantise(ahead, 0)
-            if n_back > 1:
-                add_and_store(g - 1, 1)
-            if n_ahead > 1:
-                quantise(ahead, 1)
+            for i in range(n_back):
+                add_and_store(g - 1, i)

@@ -17,9 +17,12 @@ TOKENS = 8 * 8 * 128
 PER_PARTITION = TOKENS // P
 TILES = 2
 UNIT = TILES * P
-GROUPS = ((0,),) + tuple((u, u + 1) for u in range(1, 31, 2)) + ((31,),)
+UNITS = PER_PARTITION // TILES
+GROUPS = ((0,),) + tuple((u, u + 1) for u in range(1, UNITS - 1, 2)) + ((UNITS - 1,),)
+PLACE = {a: (g, i) for g, group in enumerate(GROUPS) for i, a in enumerate(group)}
 PLAIN_TILES = 3
-LEAD = 2
+LEAD = 3
+LAG = 4
 FLOPS = 2 * TOKENS * 2 * D * 2 * D
 
 
@@ -32,12 +35,12 @@ def tile_scan_pb_t_kernel(tc, query, wc, w_lin, b_lin, w_gate, b_gate, out):
     with ExitStack() as ctx:
         ctx.enter_context(tc.manual_schedule())
         const = ctx.enter_context(tc.tile_pool(name="const", bufs=1))
-        units = PER_PARTITION // TILES
-        x_pool = ctx.enter_context(tc.tile_pool(name="x_pool", bufs=units))
-        o_pool = ctx.enter_context(tc.tile_pool(name="o_pool", bufs=units))
-        grouped_pool = ctx.enter_context(tc.tile_pool(name="grouped_pool", bufs=3))
-        packed_pool = ctx.enter_context(tc.tile_pool(name="packed_pool", bufs=LEAD + 2))
+        x_pool = ctx.enter_context(tc.tile_pool(name="x_pool", bufs=UNITS))
+        o_pool = ctx.enter_context(tc.tile_pool(name="o_pool", bufs=UNITS))
+        grouped_pool = ctx.enter_context(tc.tile_pool(name="grouped_pool", bufs=4))
+        packed_pool = ctx.enter_context(tc.tile_pool(name="packed_pool", bufs=4))
         act_pool = ctx.enter_context(tc.tile_pool(name="act_pool", bufs=3))
+        step_pool = ctx.enter_context(tc.tile_pool(name="step_pool", bufs=8))
         psum = ctx.enter_context(tc.psum_pool(name="psum", bufs=8))
 
         identity = const.tile([P, P], F32)
@@ -48,7 +51,7 @@ def tile_scan_pb_t_kernel(tc, query, wc, w_lin, b_lin, w_gate, b_gate, out):
         nc.vector.memset(bias_rows[:], 0.0)
 
         x_of = []
-        for a in range(units):
+        for a in range(UNITS):
             x = x_pool.tile([P, TILES, 2, 2, P], BF16, tag="x")
             x_of.append(x)
 
@@ -67,7 +70,7 @@ def tile_scan_pb_t_kernel(tc, query, wc, w_lin, b_lin, w_gate, b_gate, out):
                 nc.scalar.dma_start(
                     out=w_rows[64 * s : 64 * s + 64, i].rearrange("m (f e) o -> m f (e o)", f=2), in_=w_dram[s]
                 )
-        for a in range(1, units):
+        for a in range(1, UNITS):
             load_unit(a)
 
         in_bank_of = {}
@@ -75,8 +78,9 @@ def tile_scan_pb_t_kernel(tc, query, wc, w_lin, b_lin, w_gate, b_gate, out):
         packed_of = {}
         z_of = {}
         acts_of = {}
-        back_bank_of = {}
+        step_of = {}
         query_bank_of = {}
+        back_bank_of = {}
 
         def transpose_in(a):
             pairs = x_of[a][:].bitcast(F32).rearrange("p t f s w -> p t f (s w)")
@@ -86,31 +90,34 @@ def tile_scan_pb_t_kernel(tc, query, wc, w_lin, b_lin, w_gate, b_gate, out):
                     nc.tensor.transpose(in_bank[:, t, f, :], pairs[:, t, f, :], identity[:])
             in_bank_of[a] = in_bank
 
-        def copy_in(g, i):
-            if i == 0:
-                grouped_of[g] = grouped_pool.tile(
-                    [P, len(GROUPS[g]) * UNIT * 4], BF16, name="grouped", tag="grouped", align_bytes=64
-                )
-            pairs = grouped_of[g][:, i * UNIT * 4 : (i + 1) * UNIT * 4].bitcast(F32)
+        def copy_in(a):
+            grouped = grouped_pool.tile([P, UNIT * 4], BF16, tag="grouped", align_bytes=64)
             nc.scalar.copy(
-                out=pairs.rearrange("p (t n f) -> p t n f", t=TILES, f=2),
-                in_=in_bank_of[GROUPS[g][i]][:].rearrange("p t f n -> p t n f"),
+                out=grouped[:].bitcast(F32).rearrange("p (t n f) -> p t n f", t=TILES, f=2),
+                in_=in_bank_of[a][:].rearrange("p t f n -> p t n f"),
+            )
+            grouped_of[a] = grouped
+
+        def quantise(a):
+            g, i = PLACE[a]
+            if i == 0:
+                words = packed_pool.tile([P, len(GROUPS[g]) * UNIT], U32, tag="words", align_bytes=64)
+                scales = packed_pool.tile([P, len(GROUPS[g]) * UNIT], U8, tag="scales", align_bytes=64)
+                packed_of[g] = (words, scales)
+            words, scales = packed_of[g]
+            columns = slice(i * UNIT, (i + 1) * UNIT)
+            nc.vector.quantize_mx(
+                out=words[:, columns].bitcast(FP8X4), scales=scales[:, columns], in_=grouped_of[a][:]
             )
 
-        def quantise(g):
-            words = packed_pool.tile([P, len(GROUPS[g]) * UNIT], U32, tag="words", align_bytes=64)
-            scales = packed_pool.tile([P, len(GROUPS[g]) * UNIT], U8, tag="scales", align_bytes=64)
-            nc.vector.quantize_mx(out=words[:].bitcast(FP8X4), scales=scales[:], in_=grouped_of[g][:])
-            packed_of[g] = (words, scales)
-
-        def passes(g):
+        def passes(g, f):
             words, scales = packed_of[g]
-            for chunk in (0, 2, 1, 3):
+            n = len(GROUPS[g]) * UNIT
+            for chunk in (f, 2 + f):
                 z_bank = psum.tile([P, 2 * UNIT], F32, tag="bank")
-                z = z_bank[:, 0 : len(GROUPS[g]) * UNIT]
                 columns = slice(chunk * P, (chunk + 1) * P)
                 nc.tensor.matmul_mx(
-                    out=z,
+                    out=z_bank[:, 0:n],
                     lhsT=w_words[:, columns].bitcast(FP8X4),
                     lhsT_scale=w_scales[:, columns],
                     rhs=words[:].bitcast(FP8X4),
@@ -118,64 +125,57 @@ def tile_scan_pb_t_kernel(tc, query, wc, w_lin, b_lin, w_gate, b_gate, out):
                     start=True,
                     stop=True,
                 )
-                z_of[g, chunk] = z
-            h = act_pool.tile([P, 2, len(GROUPS[g]) * UNIT], F32, tag="h")
-            upd = act_pool.tile([P, 2, len(GROUPS[g]) * UNIT], F32, tag="upd")
-            diff = act_pool.tile([P, 2, len(GROUPS[g]) * UNIT], F32, tag="diff")
-            step = act_pool.tile([P, 2, len(GROUPS[g]) * UNIT], F32, tag="step")
-            acts_of[g] = (h, upd, diff, step)
+                z_of[g, chunk] = z_bank
 
-        def activate_h(g, f):
-            nc.scalar.activation(
-                out=acts_of[g][0][:, f, :],
-                in_=z_of[g, 2 + f],
-                func=ACT.Sigmoid,
-                bias=bias[:, 2 + f : 3 + f],
-                scale=-1.0,
-            )
-
-        def activate_upd(g, f):
-            nc.scalar.activation(
-                out=acts_of[g][1][:, f, :], in_=z_of[g, f], func=ACT.Tanh, bias=bias[:, f : f + 1], scale=1.0
-            )
-
-        def transpose_query(g):
-            query_bank = psum.tile([P, 2, 2 * UNIT], BF16, tag="bank")
+        def turn_query(g, f):
+            query_bank = psum.tile([P, 2 * UNIT], BF16, tag="bank")
             for i, a in enumerate(GROUPS[g]):
                 for t in range(TILES):
-                    for f in range(2):
-                        n0 = i * UNIT + t * P
-                        rows = x_of[a][:, t, f, 0, :]
-                        if i * TILES + t < PLAIN_TILES:
-                            nc.tensor.matmul(
-                                query_bank[:, f, n0 : n0 + P], lhsT=rows, rhs=identity_bf16[:], start=True, stop=True
-                            )
-                        else:
-                            nc.tensor.transpose(query_bank[:, f, n0 : n0 + P], rows, identity_bf16[:])
-            query_bank_of[g] = query_bank
+                    tile = i * TILES + t
+                    turned = query_bank[:, tile * P : (tile + 1) * P]
+                    rows = x_of[a][:, t, f, 0, :]
+                    if tile < PLAIN_TILES:
+                        nc.tensor.matmul(turned, lhsT=rows, rhs=identity_bf16[:], start=True, stop=True)
+                    else:
+                        nc.tensor.transpose(turned, rows, identity_bf16[:])
+            query_bank_of[g, f] = query_bank
+
+        def activate(g, f):
+            n = len(GROUPS[g]) * UNIT
+            upd = act_pool.tile([P, 2 * UNIT], F32, tag="upd")
+            nc.scalar.activation(
+                out=upd[:, 0:n], in_=z_of[g, f][:, 0:n], func=ACT.Tanh, bias=bias[:, f : f + 1], scale=1.0
+            )
+            h = act_pool.tile([P, 2 * UNIT], F32, tag="h")
+            nc.scalar.activation(
+                out=h[:, 0:n], in_=z_of[g, 2 + f][:, 0:n], func=ACT.Sigmoid, bias=bias[:, 2 + f : 3 + f], scale=-1.0
+            )
+            acts_of[g, f] = (upd, h)
 
         def blend(g, f):
-            h, upd, diff, step = acts_of[g]
             n = len(GROUPS[g]) * UNIT
+            upd, h = acts_of[g, f]
+            diff = act_pool.tile([P, 2 * UNIT], F32, tag="diff")
             nc.vector.tensor_tensor(
-                out=diff[:, f, :], in0=upd[:, f, :], in1=query_bank_of[g][:, f, 0:n], op=ALU.subtract
+                out=diff[:, 0:n], in0=upd[:, 0:n], in1=query_bank_of[g, f][:, 0:n], op=ALU.subtract
             )
-            nc.gpsimd.tensor_tensor(out=step[:, f, :], in0=h[:, f, :], in1=diff[:, f, :], op=ALU.mult)
+            step = step_pool.tile([P, 2 * UNIT], F32, tag="step")
+            nc.gpsimd.tensor_tensor(out=step[:, 0:n], in0=h[:, 0:n], in1=diff[:, 0:n], op=ALU.mult)
+            step_of[g, f] = step
 
-        def transpose_back(g, i):
-            step = acts_of[g][3]
+        def transpose_back(a):
+            g, i = PLACE[a]
             back_bank = psum.tile([P, 2 * TILES, P], F32, tag="bank")
             for t in range(TILES):
+                n0 = i * UNIT + t * P
                 for f in range(2):
-                    n0 = i * UNIT + t * P
-                    nc.tensor.transpose(back_bank[:, 2 * t + f, :], step[:, f, n0 : n0 + P], identity[:])
-            back_bank_of[g, i] = back_bank
+                    nc.tensor.transpose(back_bank[:, 2 * t + f, :], step_of[g, f][:, n0 : n0 + P], identity[:])
+            back_bank_of[a] = back_bank
 
-        def add_and_store(g, i):
-            a = GROUPS[g][i]
+        def add_and_store(a):
             q = x_of[a][:].rearrange("p t f s c -> p (t f) s c")[:, :, 0, :]
             o = o_pool.tile([P, 2 * TILES, P], F32, tag="o")
-            nc.vector.tensor_tensor(out=o[:], in0=back_bank_of[g, i][:], in1=q, op=ALU.add)
+            nc.vector.tensor_tensor(out=o[:], in0=back_bank_of[a][:], in1=q, op=ALU.add)
             nc.sync.dma_start(
                 out=o_dram[:, a * TILES : (a + 1) * TILES, :], in_=o[:].rearrange("p (t f) c -> p t (f c)", t=TILES)
             )
@@ -192,41 +192,34 @@ def tile_scan_pb_t_kernel(tc, query, wc, w_lin, b_lin, w_gate, b_gate, out):
         nc.vector.tensor_copy(out=bias[:, 0:2], in_=bias_bank[:, 0:2])
         nc.vector.tensor_scalar_mul(out=bias[:, 2:4], in0=bias_bank[:, 2:4], scalar1=-1.0)
         transpose_in(0)
-        copy_in(0, 0)
+        copy_in(0)
         nc.vector.tensor_copy(out=w_grouped[:], in_=w_rows[:].rearrange("p i v o -> p i o v"))
         transpose_in(1)
-        copy_in(1, 0)
+        copy_in(1)
         transpose_in(2)
-        copy_in(1, 1)
+        copy_in(2)
         nc.vector.quantize_mx(
             out=w_words[:].bitcast(FP8X4), scales=w_scales[:], in_=w_grouped[:].rearrange("p i o v -> p (i o v)")
         )
         quantise(0)
         quantise(1)
 
-        for g in range(len(GROUPS) + 1):
-            ahead = g + LEAD if g + LEAD < len(GROUPS) else None
-            n_ahead = len(GROUPS[ahead]) if ahead else 0
-            n_back = len(GROUPS[g - 1]) if g >= 1 else 0
-            now = g < len(GROUPS)
-            if now:
-                passes(g)
-                transpose_query(g)
-            for i in range(n_ahead):
-                transpose_in(GROUPS[ahead][i])
-            for i in range(n_back):
-                transpose_back(g - 1, i)
-            if now:
-                for f in range(2):
-                    activate_upd(g, f)
-                    activate_h(g, f)
-            for i in range(n_ahead):
-                copy_in(ahead, i)
-            if now:
-                blend(g, 0)
-            if 1 <= g < len(GROUPS) - 1:
-                quantise(g + 1)
-            if now:
-                blend(g, 1)
-            for i in range(n_back):
-                add_and_store(g - 1, i)
+        for k in range(UNITS + LAG):
+            g, f = divmod(k, 2)
+            if g < len(GROUPS):
+                passes(g, f)
+                turn_query(g, f)
+            if k + LEAD < UNITS:
+                transpose_in(k + LEAD)
+            if k >= LAG:
+                transpose_back(k - LAG)
+            if g < len(GROUPS):
+                activate(g, f)
+            if k + LEAD < UNITS:
+                copy_in(k + LEAD)
+            if g < len(GROUPS):
+                blend(g, f)
+            if k + LEAD - 1 < UNITS:
+                quantise(k + LEAD - 1)
+            if k >= LAG:
+                add_and_store(k - LAG)

@@ -45,10 +45,14 @@ def tile_scan_pb_t_kernel(tc, query, wc, w_lin, b_lin, w_gate, b_gate, out):
 
         identity = const.tile([P, P], F32)
         make_identity(nc, identity[:])
-        identity_bf16 = const.tile([P, P], BF16)
-        make_identity(nc, identity_bf16[:])
         bias_rows = const.tile([P, P], BF16)
         nc.vector.memset(bias_rows[:], 0.0)
+        zero_column = const.tile([P, 1], F32)
+        nc.vector.memset(zero_column[:], 0.0)
+        nc.gpsimd.dma_start(out=bias_rows[0:2, :], in_=b_lin.rearrange("(r c) -> r c", r=2))
+        nc.gpsimd.dma_start(out=bias_rows[2:4, :], in_=b_gate.rearrange("(r c) -> r c", r=2))
+        identity_bf16 = const.tile([P, P], BF16)
+        make_identity(nc, identity_bf16[:])
 
         x_of = []
         for a in range(UNITS):
@@ -61,15 +65,15 @@ def tile_scan_pb_t_kernel(tc, query, wc, w_lin, b_lin, w_gate, b_gate, out):
             nc.sync.dma_start(out=x_of[a][:, :, :, 1, :], in_=c_dram[:, tokens, :, :])
 
         load_unit(0)
-        nc.scalar.dma_start(out=bias_rows[0:2, :], in_=b_lin.rearrange("(r c) -> r c", r=2))
-        nc.scalar.dma_start(out=bias_rows[2:4, :], in_=b_gate.rearrange("(r c) -> r c", r=2))
         w_rows = const.tile([P, 2, 4, D], BF16)
-        for i, weight in enumerate((w_lin, w_gate)):
+        for i, (weight, queue) in enumerate(((w_lin, nc.scalar), (w_gate, nc.sync))):
             w_dram = weight.rearrange("(s f m e) o -> s m f (e o)", s=2, f=2, e=2)
             for s in range(2):
-                nc.scalar.dma_start(
+                queue.dma_start(
                     out=w_rows[64 * s : 64 * s + 64, i].rearrange("m (f e) o -> m f (e o)", f=2), in_=w_dram[s]
                 )
+        table_seed = const.tile([P, 1], F32)
+        nc.scalar.activation(out=table_seed[:], in_=zero_column[:], func=ACT.Sigmoid, bias=0.0, scale=1.0)
         for a in range(1, UNITS):
             load_unit(a)
 
@@ -115,7 +119,8 @@ def tile_scan_pb_t_kernel(tc, query, wc, w_lin, b_lin, w_gate, b_gate, out):
             n = len(GROUPS[g]) * UNIT
             for chunk in (f, 2 + f):
                 z_bank = psum.tile([P, 2 * UNIT], F32, tag="bank")
-                columns = slice(chunk * P, (chunk + 1) * P)
+                i, half = divmod(chunk, 2)
+                columns = slice((2 * half + i) * P, (2 * half + i + 1) * P)
                 nc.tensor.matmul_mx(
                     out=z_bank[:, 0:n],
                     lhsT=w_words[:, columns].bitcast(FP8X4),
@@ -180,45 +185,60 @@ def tile_scan_pb_t_kernel(tc, query, wc, w_lin, b_lin, w_gate, b_gate, out):
                 out=o_dram[:, a * TILES : (a + 1) * TILES, :], in_=o[:].rearrange("p (t f) c -> p t (f c)", t=TILES)
             )
 
-        w_grouped = const.tile([P, 2, D, 4], BF16, align_bytes=64)
+        w_grouped = const.tile([P, 2, 2, P, 4], BF16, align_bytes=64)
         w_words = const.tile([P, 2 * D], U32, align_bytes=64)
         w_scales = const.tile([P, 2 * D], U8, align_bytes=64)
         bias_rows_f32 = const.tile([P, P], F32)
         bias = const.tile([P, 4], F32)
 
+        def pack_weights(f, i):
+            nc.vector.tensor_copy(
+                out=w_grouped[:, f, i], in_=w_rows[:, i, :, f * P : (f + 1) * P].rearrange("p v o -> p o v")
+            )
+
+        def quantise_weights(f, i):
+            columns = slice((2 * f + i) * P, (2 * f + i + 1) * P)
+            nc.vector.quantize_mx(
+                out=w_words[:, columns].bitcast(FP8X4),
+                scales=w_scales[:, columns],
+                in_=w_grouped[:, f, i].rearrange("p o v -> p (o v)"),
+            )
+
+        transpose_in(0)
+        copy_in(0)
+        pack_weights(0, 0)
         nc.vector.tensor_copy(out=bias_rows_f32[:], in_=bias_rows[:])
         bias_bank = psum.tile([P, 4 * P], F32, tag="bank")
         nc.tensor.transpose(bias_bank[:, 0:P], bias_rows_f32[:], identity[:])
+        quantise_weights(0, 0)
+        pack_weights(0, 1)
+        quantise(0)
+        quantise_weights(0, 1)
         nc.vector.tensor_copy(out=bias[:, 0:2], in_=bias_bank[:, 0:2])
         nc.vector.tensor_scalar_mul(out=bias[:, 2:4], in0=bias_bank[:, 2:4], scalar1=-1.0)
-        transpose_in(0)
-        copy_in(0)
-        nc.vector.tensor_copy(out=w_grouped[:], in_=w_rows[:].rearrange("p i v o -> p i o v"))
-        transpose_in(1)
-        copy_in(1)
-        transpose_in(2)
-        copy_in(2)
-        nc.vector.quantize_mx(
-            out=w_words[:].bitcast(FP8X4), scales=w_scales[:], in_=w_grouped[:].rearrange("p i o v -> p (i o v)")
-        )
-        quantise(0)
-        quantise(1)
+        pack_weights(1, 0)
+        pack_weights(1, 1)
+        quantise_weights(1, 0)
+        quantise_weights(1, 1)
 
         for k in range(UNITS + LAG):
             g, f = divmod(k, 2)
+            ahead = {0: (1, 2), 1: (3, 4)}.get(k, (k + LEAD,) if k + LEAD < UNITS else ())
             if g < len(GROUPS):
                 passes(g, f)
                 turn_query(g, f)
-            if k + LEAD < UNITS:
-                transpose_in(k + LEAD)
+            for a in ahead:
+                transpose_in(a)
             if k >= LAG:
                 transpose_back(k - LAG)
             if g < len(GROUPS):
                 activate(g, f)
-            if k + LEAD < UNITS:
-                copy_in(k + LEAD)
+            for a in ahead:
+                copy_in(a)
             if g < len(GROUPS):
                 blend(g, f)
+            if k == 0:
+                quantise(1)
             if k + LEAD - 1 < UNITS:
                 quantise(k + LEAD - 1)
             if k >= LAG:

@@ -43,14 +43,12 @@ def tile_scan_pb_t_kernel(tc, query, wc, w_lin, b_lin, w_gate, b_gate, out):
         step_pool = ctx.enter_context(tc.tile_pool(name="step_pool", bufs=8))
         psum = ctx.enter_context(tc.psum_pool(name="psum", bufs=8))
 
-        identity = const.tile([P, P], F32)
-        make_identity(nc, identity[:])
         bias_rows = const.tile([P, P], BF16)
         nc.vector.memset(bias_rows[:], 0.0)
+        identity = const.tile([P, P], F32)
+        make_identity(nc, identity[:])
         zero_column = const.tile([P, 1], F32)
         nc.vector.memset(zero_column[:], 0.0)
-        nc.gpsimd.dma_start(out=bias_rows[0:2, :], in_=b_lin.rearrange("(r c) -> r c", r=2))
-        nc.gpsimd.dma_start(out=bias_rows[2:4, :], in_=b_gate.rearrange("(r c) -> r c", r=2))
         identity_bf16 = const.tile([P, P], BF16)
         make_identity(nc, identity_bf16[:])
 
@@ -64,6 +62,8 @@ def tile_scan_pb_t_kernel(tc, query, wc, w_lin, b_lin, w_gate, b_gate, out):
             nc.sync.dma_start(out=x_of[a][:, :, :, 0, :], in_=q_dram[:, tokens, :, :])
             nc.sync.dma_start(out=x_of[a][:, :, :, 1, :], in_=c_dram[:, tokens, :, :])
 
+        nc.scalar.dma_start(out=bias_rows[0:2, :], in_=b_lin.rearrange("(r c) -> r c", r=2))
+        nc.scalar.dma_start(out=bias_rows[2:4, :], in_=b_gate.rearrange("(r c) -> r c", r=2))
         load_unit(0)
         w_rows = const.tile([P, 2, 4, D], BF16)
         for i, (weight, queue) in enumerate(((w_lin, nc.scalar), (w_gate, nc.sync))):
@@ -94,9 +94,13 @@ def tile_scan_pb_t_kernel(tc, query, wc, w_lin, b_lin, w_gate, b_gate, out):
                     nc.tensor.transpose(in_bank[:, t, f, :], pairs[:, t, f, :], identity[:])
             in_bank_of[a] = in_bank
 
+        def on_vector(a):
+            return a > 4 and a % 4 == 0
+
         def copy_in(a):
             grouped = grouped_pool.tile([P, UNIT * 4], BF16, tag="grouped", align_bytes=64)
-            nc.scalar.copy(
+            copy = nc.vector.tensor_copy if on_vector(a) else nc.scalar.copy
+            copy(
                 out=grouped[:].bitcast(F32).rearrange("p (t n f) -> p t n f", t=TILES, f=2),
                 in_=in_bank_of[a][:].rearrange("p t f n -> p t n f"),
             )
@@ -132,18 +136,19 @@ def tile_scan_pb_t_kernel(tc, query, wc, w_lin, b_lin, w_gate, b_gate, out):
                 )
                 z_of[g, chunk] = z_bank
 
-        def turn_query(g, f):
-            query_bank = psum.tile([P, 2 * UNIT], BF16, tag="bank")
-            for i, a in enumerate(GROUPS[g]):
-                for t in range(TILES):
-                    tile = i * TILES + t
-                    turned = query_bank[:, tile * P : (tile + 1) * P]
-                    rows = x_of[a][:, t, f, 0, :]
-                    if tile < PLAIN_TILES:
-                        nc.tensor.matmul(turned, lhsT=rows, rhs=identity_bf16[:], start=True, stop=True)
-                    else:
-                        nc.tensor.transpose(turned, rows, identity_bf16[:])
-            query_bank_of[g, f] = query_bank
+        def turn_query(g, f, part):
+            if part == 0:
+                query_bank_of[g, f] = psum.tile([P, 2 * UNIT], BF16, name="query_bank", tag="bank")
+            tiles = [(a, t) for a in GROUPS[g] for t in range(TILES)]
+            half = len(tiles) // 2
+            for tile in range(part * half, (part + 1) * half):
+                a, t = tiles[tile]
+                turned = query_bank_of[g, f][:, tile * P : (tile + 1) * P]
+                rows = x_of[a][:, t, f, 0, :]
+                if tile < PLAIN_TILES:
+                    nc.tensor.matmul(turned, lhsT=rows, rhs=identity_bf16[:], start=True, stop=True)
+                else:
+                    nc.tensor.transpose(turned, rows, identity_bf16[:])
 
         def activate(g, f):
             n = len(GROUPS[g]) * UNIT
@@ -221,25 +226,32 @@ def tile_scan_pb_t_kernel(tc, query, wc, w_lin, b_lin, w_gate, b_gate, out):
         quantise_weights(1, 0)
         quantise_weights(1, 1)
 
+        turn_query(0, 0, 0)
         for k in range(UNITS + LAG):
             g, f = divmod(k, 2)
             ahead = {0: (1, 2), 1: (3, 4)}.get(k, (k + LEAD,) if k + LEAD < UNITS else ())
             if g < len(GROUPS):
                 passes(g, f)
-                turn_query(g, f)
+                turn_query(g, f, 1)
             for a in ahead:
                 transpose_in(a)
             if k >= LAG:
                 transpose_back(k - LAG)
+            if k + 1 < 2 * len(GROUPS):
+                turn_query((k + 1) // 2, (k + 1) % 2, 0)
             if g < len(GROUPS):
                 activate(g, f)
             for a in ahead:
-                copy_in(a)
+                if not on_vector(a):
+                    copy_in(a)
             if g < len(GROUPS):
                 blend(g, f)
             if k == 0:
                 quantise(1)
             if k + LEAD - 1 < UNITS:
                 quantise(k + LEAD - 1)
+            for a in ahead:
+                if on_vector(a):
+                    copy_in(a)
             if k >= LAG:
                 add_and_store(k - LAG)

from contextlib import ExitStack

import concourse.mybir as mybir
from concourse.masks import make_identity

F32 = mybir.dt.float32
BF16 = mybir.dt.bfloat16
U32 = mybir.dt.uint32
U8 = mybir.dt.uint8
FP8X4 = mybir.dt.float8_e4m3fn_x4
ACT = mybir.ActivationFunctionType
ALU = mybir.AluOpType

P = 128
D = 256
TOKENS = 8 * 8 * 128
PER_PARTITION = TOKENS // P
TILES = 2
UNIT = TILES * P
UNITS = PER_PARTITION // TILES
GROUPS = ((0,),) + tuple((u, u + 1) for u in range(1, UNITS - 1, 2)) + ((UNITS - 1,),)
PLACE = {a: (g, i) for g, group in enumerate(GROUPS) for i, a in enumerate(group)}
PLAIN_TILES = 3
LEAD = 3
LAG = 4
FLOPS = 2 * TOKENS * 2 * D * 2 * D


def tile_scan_pb_t_kernel(tc, query, wc, w_lin, b_lin, w_gate, b_gate, out):
    nc = tc.nc
    q_dram = query.flatten_outer_dims().rearrange("(p j) (f c) -> p j f c", j=PER_PARTITION, f=2)
    c_dram = wc.flatten_outer_dims().rearrange("(p j) (f c) -> p j f c", j=PER_PARTITION, f=2)
    o_dram = out.flatten_outer_dims().rearrange("(p j) d -> p j d", j=PER_PARTITION)

    with ExitStack() as ctx:
        ctx.enter_context(tc.manual_schedule())
        const = ctx.enter_context(tc.tile_pool(name="const", bufs=1))
        x_pool = ctx.enter_context(tc.tile_pool(name="x_pool", bufs=UNITS))
        o_pool = ctx.enter_context(tc.tile_pool(name="o_pool", bufs=UNITS))
        grouped_pool = ctx.enter_context(tc.tile_pool(name="grouped_pool", bufs=4))
        packed_pool = ctx.enter_context(tc.tile_pool(name="packed_pool", bufs=4))
        act_pool = ctx.enter_context(tc.tile_pool(name="act_pool", bufs=3))
        step_pool = ctx.enter_context(tc.tile_pool(name="step_pool", bufs=8))
        psum = ctx.enter_context(tc.psum_pool(name="psum", bufs=8))

        bias_rows = const.tile([P, P], BF16)
        nc.vector.memset(bias_rows[:], 0.0)
        identity = const.tile([P, P], F32)
        make_identity(nc, identity[:])
        zero_column = const.tile([P, 1], F32)
        nc.vector.memset(zero_column[:], 0.0)
        identity_bf16 = const.tile([P, P], BF16)
        make_identity(nc, identity_bf16[:])

        x_of = []
        for a in range(UNITS):
            x = x_pool.tile([P, TILES, 2, 2, P], BF16, tag="x")
            x_of.append(x)

        def load_unit(a):
            tokens = slice(a * TILES, (a + 1) * TILES)
            nc.sync.dma_start(out=x_of[a][:, :, :, 0, :], in_=q_dram[:, tokens, :, :])
            nc.sync.dma_start(out=x_of[a][:, :, :, 1, :], in_=c_dram[:, tokens, :, :])

        nc.scalar.dma_start(out=bias_rows[0:2, :], in_=b_lin.rearrange("(r c) -> r c", r=2))
        nc.scalar.dma_start(out=bias_rows[2:4, :], in_=b_gate.rearrange("(r c) -> r c", r=2))
        load_unit(0)
        w_rows = const.tile([P, 2, 4, D], BF16)
        for i, (weight, queue) in enumerate(((w_lin, nc.scalar), (w_gate, nc.sync))):
            w_dram = weight.rearrange("(s f m e) o -> s m f (e o)", s=2, f=2, e=2)
            for s in range(2):
                queue.dma_start(
                    out=w_rows[64 * s : 64 * s + 64, i].rearrange("m (f e) o -> m f (e o)", f=2), in_=w_dram[s]
                )
        table_seed = const.tile([P, 1], F32)
        nc.scalar.activation(out=table_seed[:], in_=zero_column[:], func=ACT.Sigmoid, bias=0.0, scale=1.0)
        for a in range(1, UNITS):
            load_unit(a)

        in_bank_of = {}
        grouped_of = {}
        packed_of = {}
        z_of = {}
        acts_of = {}
        step_of = {}
        query_bank_of = {}
        back_bank_of = {}

        def transpose_in(a):
            pairs = x_of[a][:].bitcast(F32).rearrange("p t f s w -> p t f (s w)")
            in_bank = psum.tile([P, TILES, 2, P], F32, tag="bank")
            for t in range(TILES):
                for f in range(2):
                    nc.tensor.transpose(in_bank[:, t, f, :], pairs[:, t, f, :], identity[:])
            in_bank_of[a] = in_bank

        def on_vector(a):
            return a > 4 and a % 4 == 0

        def copy_in(a):
            grouped = grouped_pool.tile([P, UNIT * 4], BF16, tag="grouped", align_bytes=64)
            copy = nc.vector.tensor_copy if on_vector(a) else nc.scalar.copy
            copy(
                out=grouped[:].bitcast(F32).rearrange("p (t n f) -> p t n f", t=TILES, f=2),
                in_=in_bank_of[a][:].rearrange("p t f n -> p t n f"),
            )
            grouped_of[a] = grouped

        def quantise(a):
            g, i = PLACE[a]
            if i == 0:
                words = packed_pool.tile([P, len(GROUPS[g]) * UNIT], U32, tag="words", align_bytes=64)
                scales = packed_pool.tile([P, len(GROUPS[g]) * UNIT], U8, tag="scales", align_bytes=64)
                packed_of[g] = (words, scales)
            words, scales = packed_of[g]
            columns = slice(i * UNIT, (i + 1) * UNIT)
            nc.vector.quantize_mx(
                out=words[:, columns].bitcast(FP8X4), scales=scales[:, columns], in_=grouped_of[a][:]
            )

        def passes(g, f):
            words, scales = packed_of[g]
            n = len(GROUPS[g]) * UNIT
            for chunk in (f, 2 + f):
                z_bank = psum.tile([P, 2 * UNIT], F32, tag="bank")
                i, half = divmod(chunk, 2)
                columns = slice((2 * half + i) * P, (2 * half + i + 1) * P)
                nc.tensor.matmul_mx(
                    out=z_bank[:, 0:n],
                    lhsT=w_words[:, columns].bitcast(FP8X4),
                    lhsT_scale=w_scales[:, columns],
                    rhs=words[:].bitcast(FP8X4),
                    rhs_scale=scales[:],
                    start=True,
                    stop=True,
                )
                z_of[g, chunk] = z_bank

        def turn_query(g, f, part):
            if part == 0:
                query_bank_of[g, f] = psum.tile([P, 2 * UNIT], BF16, name="query_bank", tag="bank")
            tiles = [(a, t) for a in GROUPS[g] for t in range(TILES)]
            half = len(tiles) // 2
            for tile in range(part * half, (part + 1) * half):
                a, t = tiles[tile]
                turned = query_bank_of[g, f][:, tile * P : (tile + 1) * P]
                rows = x_of[a][:, t, f, 0, :]
                if tile < PLAIN_TILES:
                    nc.tensor.matmul(turned, lhsT=rows, rhs=identity_bf16[:], start=True, stop=True)
                else:
                    nc.tensor.transpose(turned, rows, identity_bf16[:])

        def activate(g, f):
            n = len(GROUPS[g]) * UNIT
            upd = act_pool.tile([P, 2 * UNIT], F32, tag="upd")
            nc.scalar.activation(
                out=upd[:, 0:n], in_=z_of[g, f][:, 0:n], func=ACT.Tanh, bias=bias[:, f : f + 1], scale=1.0
            )
            h = act_pool.tile([P, 2 * UNIT], F32, tag="h")
            nc.scalar.activation(
                out=h[:, 0:n], in_=z_of[g, 2 + f][:, 0:n], func=ACT.Sigmoid, bias=bias[:, 2 + f : 3 + f], scale=-1.0
            )
            acts_of[g, f] = (upd, h)

        def blend(g, f):
            n = len(GROUPS[g]) * UNIT
            upd, h = acts_of[g, f]
            diff = act_pool.tile([P, 2 * UNIT], F32, tag="diff")
            nc.vector.tensor_tensor(
                out=diff[:, 0:n], in0=upd[:, 0:n], in1=query_bank_of[g, f][:, 0:n], op=ALU.subtract
            )
            step = step_pool.tile([P, 2 * UNIT], F32, tag="step")
            nc.gpsimd.tensor_tensor(out=step[:, 0:n], in0=h[:, 0:n], in1=diff[:, 0:n], op=ALU.mult)
            step_of[g, f] = step

        def transpose_back(a):
            g, i = PLACE[a]
            back_bank = psum.tile([P, 2 * TILES, P], F32, tag="bank")
            for t in range(TILES):
                n0 = i * UNIT + t * P
                for f in range(2):
                    nc.tensor.transpose(back_bank[:, 2 * t + f, :], step_of[g, f][:, n0 : n0 + P], identity[:])
            back_bank_of[a] = back_bank

        def add_and_store(a):
            q = x_of[a][:].rearrange("p t f s c -> p (t f) s c")[:, :, 0, :]
            o = o_pool.tile([P, 2 * TILES, P], F32, tag="o")
            nc.vector.tensor_tensor(out=o[:], in0=back_bank_of[a][:], in1=q, op=ALU.add)
            nc.sync.dma_start(
                out=o_dram[:, a * TILES : (a + 1) * TILES, :], in_=o[:].rearrange("p (t f) c -> p t (f c)", t=TILES)
            )

        w_grouped = const.tile([P, 2, 2, P, 4], BF16, align_bytes=64)
        w_words = const.tile([P, 2 * D], U32, align_bytes=64)
        w_scales = const.tile([P, 2 * D], U8, align_bytes=64)
        bias_rows_f32 = const.tile([P, P], F32)
        bias = const.tile([P, 4], F32)

        def pack_weights(f, i):
            nc.vector.tensor_copy(
                out=w_grouped[:, f, i], in_=w_rows[:, i, :, f * P : (f + 1) * P].rearrange("p v o -> p o v")
            )

        def quantise_weights(f, i):
            columns = slice((2 * f + i) * P, (2 * f + i + 1) * P)
            nc.vector.quantize_mx(
                out=w_words[:, columns].bitcast(FP8X4),
                scales=w_scales[:, columns],
                in_=w_grouped[:, f, i].rearrange("p o v -> p (o v)"),
            )

        transpose_in(0)
        copy_in(0)
        pack_weights(0, 0)
        nc.vector.tensor_copy(out=bias_rows_f32[:], in_=bias_rows[:])
        bias_bank = psum.tile([P, 4 * P], F32, tag="bank")
        nc.tensor.transpose(bias_bank[:, 0:P], bias_rows_f32[:], identity[:])
        quantise_weights(0, 0)
        pack_weights(0, 1)
        quantise(0)
        quantise_weights(0, 1)
        nc.vector.tensor_copy(out=bias[:, 0:2], in_=bias_bank[:, 0:2])
        nc.vector.tensor_scalar_mul(out=bias[:, 2:4], in0=bias_bank[:, 2:4], scalar1=-1.0)
        pack_weights(1, 0)
        pack_weights(1, 1)
        quantise_weights(1, 0)
        quantise_weights(1, 1)

        turn_query(0, 0, 0)
        for k in range(UNITS + LAG):
            g, f = divmod(k, 2)
            ahead = {0: (1, 2), 1: (3, 4)}.get(k, (k + LEAD,) if k + LEAD < UNITS else ())
            if g < len(GROUPS):
                passes(g, f)
                turn_query(g, f, 1)
            for a in ahead:
                transpose_in(a)
            if k >= LAG:
                transpose_back(k - LAG)
            if k + 1 < 2 * len(GROUPS):
                turn_query((k + 1) // 2, (k + 1) % 2, 0)
            if g < len(GROUPS):
                activate(g, f)
            for a in ahead:
                if not on_vector(a):
                    copy_in(a)
            if g < len(GROUPS):
                blend(g, f)
            if k == 0:
                quantise(1)
            if k + LEAD - 1 < UNITS:
                quantise(k + LEAD - 1)
            for a in ahead:
                if on_vector(a):
                    copy_in(a)
            if k >= LAG:
                add_and_store(k - LAG)
